import numpy as np
import ml_dtypes


def mxq(x, axis, fmt="e4m3"):
    dtype, down = {"e4m3": (ml_dtypes.float8_e4m3fn, 7), "e5m2": (ml_dtypes.float8_e5m2, 14)}[fmt]
    v = np.moveaxis(np.asarray(x, np.float32).astype(ml_dtypes.bfloat16).astype(np.float64), axis, -1)
    blocks = v.reshape(v.shape[:-1] + (-1, 32))
    amax = np.abs(blocks).max(-1, keepdims=True)
    byte = np.maximum(np.where(amax > 0, np.frexp(amax)[1] - 1 + 127, 0) - down, 1)
    scale = np.exp2(byte - 127.0)
    codes = (blocks / scale).astype(np.float32).astype(dtype).astype(np.float64)
    return np.moveaxis((codes * scale).reshape(v.shape), -1, axis)


WIDE = False


def mx_kscale(k):
    if not WIDE:
        return np.ones(k)
    levels = np.array([10, -10, 5, -5, 0])
    a = np.random.permutation(np.resize(levels, k // 512 * 4)).reshape(k // 512, 4)
    idx = np.arange(k)
    return np.exp2(a[idx // 512, idx % 128 // 32])


BF16 = ml_dtypes.bfloat16


def bf(x):
    return np.asarray(x, np.float32).astype(BF16)


def f64(x):
    return np.asarray(x).astype(np.float64)


B, C, H, W = 2, 512, 64, 64
C2 = C + C


def setup_inputs():
    s = mx_kscale(C)
    return {"x": bf(np.random.standard_normal((B, C, H, W)) * s[None, :, None, None]),
            "mask": bf(np.random.random_sample((B, 1, H, W))),
            "W_kv": bf(np.random.standard_normal((C, C2)) / np.sqrt(C) / s[:, None]),
            "b_kv": bf(np.random.standard_normal(C2) * 0.3)}


def reference(x, mask, W_kv, b_kv):
    x, mask = f64(x), f64(mask)
    b, c, h, w = x.shape
    xf = np.transpose(x, (0, 2, 3, 1)).reshape(b, h * w, c)
    kv = (mxq(xf, 2, "e4m3") @ mxq(f64(W_kv), 0, "e4m3")) + f64(b_kv)
    k, v = kv[..., :c], kv[..., c:]
    k = k / np.linalg.norm(k, axis=-1, keepdims=True)
    m = np.transpose(mask, (0, 2, 3, 1)).reshape(b, h * w, 1)
    inv = 1.0 - m
    ku = k * inv
    km = k * m
    kv_know = np.sum(ku * v, axis=-2, keepdims=True)
    kv_mask = np.sum(km * v, axis=-2, keepdims=True)
    return kv_know, kv_mask

@@ -1,0 +1,193 @@
+from contextlib import ExitStack
+
+import concourse.bass as bass
+import concourse.mybir as mybir
+import concourse.tile as tile
+from concourse.masks import make_identity
+
+F32 = mybir.dt.float32
+BF16 = mybir.dt.bfloat16
+U32 = mybir.dt.uint32
+U8 = mybir.dt.uint8
+FP8X4 = mybir.dt.float8_e4m3fn_x4
+ALU = mybir.AluOpType
+ACT = mybir.ActivationFunctionType
+AX = mybir.AxisListType
+
+P = 128
+PACK = 4
+B = 2
+C = 512
+T = 4096
+NT = B * T // P
+LAG = 2
+FLOPS = 2 * B * T * C * (2 * C)
+
+CHUNKS = [(0, 0, 256), (0, 256, 256), (0, 512, 512), (0, 1024, 1024), (0, 2048, 1024), (0, 3072, 1024),
+          (1, 0, 1024), (1, 1024, 1024), (1, 2048, 1024), (1, 3072, 1024)]
+
+
+PIECE = 256
+
+
+def tile_hydraattention_pa_t_kernel(tc, x, mask, W_kv, b_kv, out_0, out_1):
+    nc = tc.nc
+    with ExitStack() as ctx:
+        const = ctx.enter_context(tc.tile_pool(name="const", bufs=1))
+        stage = ctx.enter_context(tc.tile_pool(name="stage", bufs=2))
+        work = ctx.enter_context(tc.tile_pool(name="work", bufs=4))
+        prod = ctx.enter_context(tc.tile_pool(name="prod", bufs=LAG + 3))
+        psum = ctx.enter_context(tc.psum_pool(name="psum", bufs=3))
+        psum1 = ctx.enter_context(tc.psum_pool(name="psum1", bufs=1))
+        ctx.enter_context(tc.manual_schedule())
+
+        w_raw = const.tile([P, PACK, 2 * C], BF16)
+        x_raw = const.tile([P, B, PACK, T], BF16)
+        nc.sync.dma_start(out=x_raw[:, 0, :, 0:256],
+                          in_=x[0].rearrange("(p j) h w -> p j (h w)", j=PACK)[:, :, 0:256])
+        for h in range(2):
+            nc.sync.dma_start(out=w_raw[:, :, h * C:(h + 1) * C],
+                              in_=W_kv.rearrange("(p j) n -> p j n", j=PACK)[:, :, h * C:(h + 1) * C])
+        for (b, c0, wc) in CHUNKS[1:]:
+            nc.sync.dma_start(out=x_raw[:, b, :, c0:c0 + wc],
+                              in_=x[b].rearrange("(p j) h w -> p j (h w)", j=PACK)[:, :, c0:c0 + wc])
+        bias_b = const.tile([P, 2 * C], BF16)
+        nc.scalar.dma_start(out=bias_b[:], in_=b_kv.partition_broadcast(P))
+        mk_raw = const.tile([P, P], BF16)
+        nc.vector.memset(mk_raw[:], 0.0)
+        nc.scalar.dma_start(out=mk_raw[0:NT, :],
+                            in_=mask.rearrange("b o (i h) w -> (b o i) (h w)", h=2))
+
+        warm = const.tile([P, 1], F32)
+        nc.vector.memset(warm[:], 1.0)
+        nc.scalar.activation(out=warm[:], in_=warm[:], func=ACT.Sqrt)
+        ident = const.tile([P, P], F32)
+        make_identity(nc, ident[:])
+        res = const.tile([P, P], F32)
+        nc.vector.memset(res[:], 0.0)
+
+        w_grp = const.tile([P, 2 * C, PACK], BF16, align_bytes=64)
+        w_codes = const.tile([P, 2 * C], U32, align_bytes=64)
+        w_scales = const.tile([P, 2 * C], U8, align_bytes=64)
+        x_codes = const.tile([P, B * T], U32, align_bytes=64)
+        x_scales = const.tile([P, B * T], U8, align_bytes=64)
+        grps = {}
+
+        def regroup_piece(ci, s):
+            b, c0, wc = CHUNKS[ci]
+            if s == 0:
+                grps[ci] = stage.tile([P, 1024, PACK], BF16, align_bytes=64, tag="grp", name="grp")
+            grp = grps[ci]
+            nc.scalar.copy(
+                out=grp[:, s:s + PIECE, :].rearrange("p (c i) t -> p c t i", i=4),
+                in_=x_raw[:, b, :, c0 + s:c0 + s + PIECE].rearrange("p t (c i) -> p c t i", i=4))
+
+        def quantise_chunk(ci):
+            b, c0, wc = CHUNKS[ci]
+            g0 = b * T + c0
+            nc.vector.quantize_mx(
+                out=x_codes[:, g0:g0 + wc].bitcast(FP8X4),
+                scales=x_scales[:, g0:g0 + wc],
+                in_=grps[ci][:, 0:wc, :].rearrange("p w j -> p (w j)"))
+
+        regroup_piece(0, 0)
+        nc.vector.tensor_copy(
+            out=w_grp[:, 0:C, :].rearrange("p (c i) t -> p c t i", i=4),
+            in_=w_raw[:, :, 0:C].rearrange("p t (c i) -> p c t i", i=4))
+        nc.scalar.copy(
+            out=w_grp[:, C:2 * C, :].rearrange("p (c i) t -> p c t i", i=4),
+            in_=w_raw[:, :, C:2 * C].rearrange("p t (c i) -> p c t i", i=4))
+        regroup_piece(1, 0)
+        quantise_chunk(0)
+        for h in range(2):
+            nc.vector.quantize_mx(
+                out=w_codes[:, h * C:(h + 1) * C].bitcast(FP8X4),
+                scales=w_scales[:, h * C:(h + 1) * C],
+                in_=w_grp[:, h * C:(h + 1) * C, :].rearrange("p w j -> p (w j)"))
+        quantise_chunk(1)
+
+        piece_at = {}
+        quant_at = {}
+        for ci in range(2, len(CHUNKS)):
+            b, c0, wc = CHUNKS[ci]
+            first = (b * T + c0) // P
+            n_pieces = wc // PIECE
+            begin = 0 if ci == 2 else (2 if ci == 3 else first - 8)
+            for k in range(n_pieces):
+                piece_at[begin + k] = (ci, k * PIECE)
+            quant_at[begin + n_pieces + (0 if ci <= 3 else 2)] = ci
+
+        mk_f = const.tile([P, P], F32)
+        mo = const.tile([P, NT, 2], F32)
+        n2 = const.tile([P, NT], F32)
+        nrm = const.tile([P, NT], F32)
+        rn = const.tile([P, NT], F32)
+        w_t = const.tile([P, NT, 2], F32)
+        red = psum1.tile([P, NT * 4 * 2], F32, tag="red")
+        prods = {}
+
+        def front(i):
+            t0 = i * P
+            kps = psum.tile([P, C], F32, tag="kps")
+            vps = psum.tile([P, C], F32, tag="vps")
+            for h, acc in ((0, kps), (1, vps)):
+                nc.tensor.matmul_mx(
+                    out=acc[:],
+                    lhsT=x_codes[:, t0:t0 + P].bitcast(FP8X4),
+                    lhsT_scale=x_scales[:, t0:t0 + P],
+                    rhs=w_codes[:, h * C:(h + 1) * C].bitcast(FP8X4),
+                    rhs_scale=w_scales[:, h * C:(h + 1) * C],
+                    start=True, stop=True)
+            k_sb = work.tile([P, C], F32, tag="k_sb")
+            nc.vector.tensor_tensor(out=k_sb[:], in0=kps[:], in1=bias_b[:, 0:C], op=ALU.add)
+            junk = work.tile([P, C], BF16, tag="junk")
+            nc.scalar.activation(out=junk[:], in_=k_sb[:], func=ACT.Square, accum_out=n2[:, i:i + 1])
+            v_sb = work.tile([P, C], F32, tag="v_sb")
+            nc.vector.tensor_tensor(out=v_sb[:], in0=vps[:], in1=bias_b[:, C:2 * C], op=ALU.add)
+            p_sb = prod.tile([P, C], F32, tag="p_sb")
+            nc.gpsimd.tensor_tensor(out=p_sb[:], in0=k_sb[:], in1=v_sb[:], op=ALU.mult)
+            prods[i] = p_sb
+
+        def back(i):
+            p_sb = prods[i]
+            for q in range(4):
+                col = (i * 4 + q) * 2
+                nc.tensor.matmul(out=red[:, col:col + 2], lhsT=p_sb[:, q * P:(q + 1) * P],
+                                 rhs=w_t[:, i, :], start=True, stop=True)
+
+        def weights(i):
+            nc.vector.reciprocal(out=rn[:, i:i + 1], in_=nrm[:, i:i + 1])
+            nc.vector.tensor_scalar_mul(out=w_t[:, i, :], in0=mo[:, i, :], scalar1=rn[:, i:i + 1])
+
+        for i in range(NT + LAG):
+            if i == 0:
+                nc.vector.tensor_copy(out=mk_f[:], in_=mk_raw[:])
+                mk_ps = psum1.tile([P, P], F32, tag="misc")
+                nc.tensor.transpose(mk_ps[:], mk_f[:], ident[:])
+            if i < NT:
+                front(i)
+                nc.scalar.activation(out=nrm[:, i:i + 1], in_=n2[:, i:i + 1], func=ACT.Sqrt)
+                if i in piece_at:
+                    regroup_piece(piece_at[i][0], piece_at[i][1])
+                if i in quant_at:
+                    quantise_chunk(quant_at[i])
+            if i == 0:
+                nc.vector.tensor_copy(out=mo[:, :, 1], in_=mk_ps[:, 0:NT])
+                nc.vector.tensor_scalar(out=mo[:, :, 0], in0=mk_ps[:, 0:NT], scalar1=-1.0, scalar2=1.0,
+                                        op0=ALU.mult, op1=ALU.add)
+            if 1 <= i <= NT:
+                weights(i - 1)
+            if i >= LAG:
+                back(i - LAG)
+
+        for b in range(B):
+            nc.vector.tensor_reduce(
+                out=res[:, 0:16].rearrange("p (j b q) -> p j b q", j=2, b=B)[:, :, b, :],
+                in_=red[:, b * 256:(b + 1) * 256].rearrange("p (i q j) -> p j q i", q=4, j=2),
+                axis=AX.X, op=ALU.add)
+        res_ps = psum1.tile([P, P], F32, tag="misc")
+        nc.tensor.transpose(res_ps[:], res[:], ident[:])
+        res_t = const.tile([16, P], F32)
+        nc.scalar.copy(out=res_t[:], in_=res_ps[0:16, :])
+        nc.sync.dma_start(out=out_0.rearrange("b o (q p) -> (b o q) p", p=P), in_=res_t[0:8, :])
+        nc.sync.dma_start(out=out_1.rearrange("b o (q p) -> (b o q) p", p=P), in_=res_t[8:16, :])

@@ -21,6 +21,7 @@ C = 512
 T = 4096
 NT = B * T // P
 LAG = 2
+NW = 64
 FLOPS = 2 * B * T * C * (2 * C)
 
 CHUNKS = [(0, 0, 256), (0, 256, 256), (0, 512, 512), (0, 1024, 1024), (0, 2048, 1024), (0, 3072, 1024),
@@ -41,16 +42,20 @@ def tile_hydraattention_pa_t_kernel(tc, x, mask, W_kv, b_kv, out_0, out_1):
         psum1 = ctx.enter_context(tc.psum_pool(name="psum1", bufs=1))
         ctx.enter_context(tc.manual_schedule())
 
-        w_raw = const.tile([P, PACK, 2 * C], BF16)
-        x_raw = const.tile([P, B, PACK, T], BF16)
-        nc.sync.dma_start(out=x_raw[:, 0, :, 0:256],
-                          in_=x[0].rearrange("(p j) h w -> p j (h w)", j=PACK)[:, :, 0:256])
-        for h in range(2):
-            nc.sync.dma_start(out=w_raw[:, :, h * C:(h + 1) * C],
-                              in_=W_kv.rearrange("(p j) n -> p j n", j=PACK)[:, :, h * C:(h + 1) * C])
-        for (b, c0, wc) in CHUNKS[1:]:
-            nc.sync.dma_start(out=x_raw[:, b, :, c0:c0 + wc],
+        w_raw = [const.tile([P, PACK, C], BF16, name="w_raw%d" % h) for h in range(2)]
+        x_raw = [const.tile([P, PACK, wc], BF16, name="x_raw%d" % ci) for ci, (b, c0, wc) in enumerate(CHUNKS)]
+
+        def load_x(ci):
+            b, c0, wc = CHUNKS[ci]
+            nc.sync.dma_start(out=x_raw[ci][:],
                               in_=x[b].rearrange("(p j) h w -> p j (h w)", j=PACK)[:, :, c0:c0 + wc])
+
+        load_x(0)
+        for h in range(2):
+            nc.sync.dma_start(out=w_raw[h][:],
+                              in_=W_kv.rearrange("(p j) n -> p j n", j=PACK)[:, :, h * C:(h + 1) * C])
+        for ci in range(1, len(CHUNKS)):
+            load_x(ci)
         bias_b = const.tile([P, 2 * C], BF16)
         nc.scalar.dma_start(out=bias_b[:], in_=b_kv.partition_broadcast(P))
         mk_raw = const.tile([P, P], BF16)
@@ -80,7 +85,7 @@ def tile_hydraattention_pa_t_kernel(tc, x, mask, W_kv, b_kv, out_0, out_1):
             grp = grps[ci]
             nc.scalar.copy(
                 out=grp[:, s:s + PIECE, :].rearrange("p (c i) t -> p c t i", i=4),
-                in_=x_raw[:, b, :, c0 + s:c0 + s + PIECE].rearrange("p t (c i) -> p c t i", i=4))
+                in_=x_raw[ci][:, :, s:s + PIECE].rearrange("p t (c i) -> p c t i", i=4))
 
         def quantise_chunk(ci):
             b, c0, wc = CHUNKS[ci]
@@ -93,10 +98,10 @@ def tile_hydraattention_pa_t_kernel(tc, x, mask, W_kv, b_kv, out_0, out_1):
         regroup_piece(0, 0)
         nc.vector.tensor_copy(
             out=w_grp[:, 0:C, :].rearrange("p (c i) t -> p c t i", i=4),
-            in_=w_raw[:, :, 0:C].rearrange("p t (c i) -> p c t i", i=4))
+            in_=w_raw[0][:].rearrange("p t (c i) -> p c t i", i=4))
         nc.scalar.copy(
             out=w_grp[:, C:2 * C, :].rearrange("p (c i) t -> p c t i", i=4),
-            in_=w_raw[:, :, C:2 * C].rearrange("p t (c i) -> p c t i", i=4))
+            in_=w_raw[1][:].rearrange("p t (c i) -> p c t i", i=4))
         regroup_piece(1, 0)
         quantise_chunk(0)
         for h in range(2):
@@ -122,8 +127,9 @@ def tile_hydraattention_pa_t_kernel(tc, x, mask, W_kv, b_kv, out_0, out_1):
         n2 = const.tile([P, NT], F32)
         nrm = const.tile([P, NT], F32)
         rn = const.tile([P, NT], F32)
-        w_t = const.tile([P, NT, 2], F32)
-        red = psum1.tile([P, NT * 4 * 2], F32, tag="red")
+        w_t = const.tile([P, NT, NW], F32)
+        nc.gpsimd.memset(w_t[:], 0.0)
+        reds = [psum1.tile([P, 4, NW], F32, tag="red0", name="red0"), psum1.tile([P, 4, NW], F32, tag="red1", name="red1")]
         prods = {}
 
         def front(i):
@@ -150,20 +156,22 @@ def tile_hydraattention_pa_t_kernel(tc, x, mask, W_kv, b_kv, out_0, out_1):
 
         def back(i):
             p_sb = prods[i]
+            b = i // (NT // B)
+            ib = i % (NT // B)
             for q in range(4):
-                col = (i * 4 + q) * 2
-                nc.tensor.matmul(out=red[:, col:col + 2], lhsT=p_sb[:, q * P:(q + 1) * P],
-                                 rhs=w_t[:, i, :], start=True, stop=True)
+                nc.tensor.matmul(out=reds[b][:, q, :], lhsT=p_sb[:, q * P:(q + 1) * P],
+                                 rhs=w_t[:, i, :], start=(ib == 0 and q == 0),
+                                 stop=(ib == NT // B - 1 and q == 3))
 
         def weights(i):
             nc.vector.reciprocal(out=rn[:, i:i + 1], in_=nrm[:, i:i + 1])
-            nc.vector.tensor_scalar_mul(out=w_t[:, i, :], in0=mo[:, i, :], scalar1=rn[:, i:i + 1])
+            nc.vector.tensor_scalar_mul(out=w_t[:, i, 0:2], in0=mo[:, i, :], scalar1=rn[:, i:i + 1])
 
         for i in range(NT + LAG):
             if i == 0:
                 nc.vector.tensor_copy(out=mk_f[:], in_=mk_raw[:])
-                mk_ps = psum1.tile([P, P], F32, tag="misc")
-                nc.tensor.transpose(mk_ps[:], mk_f[:], ident[:])
+                mk_ps = psum.tile([P, C], F32, tag="kps", name="mk_ps")
+                nc.tensor.transpose(mk_ps[:, 0:P], mk_f[:], ident[:])
             if i < NT:
                 front(i)
                 nc.scalar.activation(out=nrm[:, i:i + 1], in_=n2[:, i:i + 1], func=ACT.Sqrt)
@@ -181,13 +189,12 @@ def tile_hydraattention_pa_t_kernel(tc, x, mask, W_kv, b_kv, out_0, out_1):
                 back(i - LAG)
 
         for b in range(B):
-            nc.vector.tensor_reduce(
+            nc.vector.tensor_copy(
                 out=res[:, 0:16].rearrange("p (j b q) -> p j b q", j=2, b=B)[:, :, b, :],
-                in_=red[:, b * 256:(b + 1) * 256].rearrange("p (i q j) -> p j q i", q=4, j=2),
-                axis=AX.X, op=ALU.add)
-        res_ps = psum1.tile([P, P], F32, tag="misc")
-        nc.tensor.transpose(res_ps[:], res[:], ident[:])
+                in_=reds[b][:, :, 0:2].rearrange("p q j -> p j q"))
+        res_ps = psum.tile([P, C], F32, tag="kps", name="res_ps")
+        nc.tensor.transpose(res_ps[:, 0:P], res[:], ident[:])
         res_t = const.tile([16, P], F32)
-        nc.scalar.copy(out=res_t[:], in_=res_ps[0:16, :])
+        nc.scalar.copy(out=res_t[:], in_=res_ps[0:16, 0:P])
         nc.sync.dma_start(out=out_0.rearrange("b o (q p) -> (b o q) p", p=P), in_=res_t[0:8, :])
         nc.sync.dma_start(out=out_1.rearrange("b o (q p) -> (b o q) p", p=P), in_=res_t[8:16, :])

@@ -20,7 +20,8 @@ B = 2
 C = 512
 T = 4096
 NT = B * T // P
-LAG = 2
+GROUPS = [4] * 15 + [2, 1, 1]
+PROD_BUFS = 12
 NW = 64
 FLOPS = 2 * B * T * C * (2 * C)
 
@@ -37,7 +38,7 @@ def tile_hydraattention_pa_t_kernel(tc, x, mask, W_kv, b_kv, out_0, out_1):
         const = ctx.enter_context(tc.tile_pool(name="const", bufs=1))
         stage = ctx.enter_context(tc.tile_pool(name="stage", bufs=2))
         work = ctx.enter_context(tc.tile_pool(name="work", bufs=4))
-        prod = ctx.enter_context(tc.tile_pool(name="prod", bufs=LAG + 3))
+        prod = ctx.enter_context(tc.tile_pool(name="prod", bufs=PROD_BUFS))
         psum = ctx.enter_context(tc.psum_pool(name="psum", bufs=3))
         psum1 = ctx.enter_context(tc.psum_pool(name="psum1", bufs=1))
         ctx.enter_context(tc.manual_schedule())
@@ -132,7 +133,29 @@ def tile_hydraattention_pa_t_kernel(tc, x, mask, W_kv, b_kv, out_0, out_1):
         reds = [psum1.tile([P, 4, NW], F32, tag="red0", name="red0"), psum1.tile([P, 4, NW], F32, tag="red1", name="red1")]
         prods = {}
 
-        def front(i):
+        def back(i):
+            p_sb = prods[i]
+            b = i // (NT // B)
+            ib = i % (NT // B)
+            for q in range(4):
+                nc.tensor.matmul(out=reds[b][:, q, :], lhsT=p_sb[:, q * P:(q + 1) * P],
+                                 rhs=w_t[:, i, :], start=(ib == 0 and q == 0),
+                                 stop=(ib == NT // B - 1 and q == 3))
+
+        sqrt_at = {}
+        weights_at = {}
+        back_at = {}
+        first = 0
+        for n in GROUPS:
+            last = first + n - 1
+            sqrt_at[last + 1] = (first, n)
+            weights_at[last + 3] = (first, n)
+            for k in range(n):
+                back_at[last + 5 + k] = back_at.get(last + 5 + k, []) + [first + k]
+            first += n
+        n_steps = max(back_at) + 1
+
+        def front_k(i):
             t0 = i * P
             kps = psum.tile([P, C], F32, tag="kps")
             vps = psum.tile([P, C], F32, tag="vps")
@@ -148,45 +171,44 @@ def tile_hydraattention_pa_t_kernel(tc, x, mask, W_kv, b_kv, out_0, out_1):
             nc.vector.tensor_tensor(out=k_sb[:], in0=kps[:], in1=bias_b[:, 0:C], op=ALU.add)
             junk = work.tile([P, C], BF16, tag="junk")
             nc.scalar.activation(out=junk[:], in_=k_sb[:], func=ACT.Square, accum_out=n2[:, i:i + 1])
+            return k_sb, vps
+
+        def front_v(i, k_sb, vps):
             v_sb = work.tile([P, C], F32, tag="v_sb")
             nc.vector.tensor_tensor(out=v_sb[:], in0=vps[:], in1=bias_b[:, C:2 * C], op=ALU.add)
             p_sb = prod.tile([P, C], F32, tag="p_sb")
             nc.gpsimd.tensor_tensor(out=p_sb[:], in0=k_sb[:], in1=v_sb[:], op=ALU.mult)
             prods[i] = p_sb
 
-        def back(i):
-            p_sb = prods[i]
-            b = i // (NT // B)
-            ib = i % (NT // B)
-            for q in range(4):
-                nc.tensor.matmul(out=reds[b][:, q, :], lhsT=p_sb[:, q * P:(q + 1) * P],
-                                 rhs=w_t[:, i, :], start=(ib == 0 and q == 0),
-                                 stop=(ib == NT // B - 1 and q == 3))
-
-        def weights(i):
-            nc.vector.reciprocal(out=rn[:, i:i + 1], in_=nrm[:, i:i + 1])
-            nc.vector.tensor_scalar_mul(out=w_t[:, i, 0:2], in0=mo[:, i, :], scalar1=rn[:, i:i + 1])
-
-        for i in range(NT + LAG):
+        for i in range(n_steps):
             if i == 0:
                 nc.vector.tensor_copy(out=mk_f[:], in_=mk_raw[:])
                 mk_ps = psum.tile([P, C], F32, tag="kps", name="mk_ps")
                 nc.tensor.transpose(mk_ps[:, 0:P], mk_f[:], ident[:])
             if i < NT:
-                front(i)
-                nc.scalar.activation(out=nrm[:, i:i + 1], in_=n2[:, i:i + 1], func=ACT.Sqrt)
-                if i in piece_at:
-                    regroup_piece(piece_at[i][0], piece_at[i][1])
-                if i in quant_at:
-                    quantise_chunk(quant_at[i])
+                k_sb, vps = front_k(i)
+            if i in weights_at:
+                f, n = weights_at[i]
+                nc.vector.reciprocal(out=rn[:, f:f + n], in_=nrm[:, f:f + n])
+            if i < NT:
+                front_v(i, k_sb, vps)
+            if i in sqrt_at:
+                f, n = sqrt_at[i]
+                nc.scalar.activation(out=nrm[:, f:f + n], in_=n2[:, f:f + n], func=ACT.Sqrt)
+            if i in piece_at:
+                regroup_piece(piece_at[i][0], piece_at[i][1])
+            if i in quant_at:
+                quantise_chunk(quant_at[i])
             if i == 0:
                 nc.vector.tensor_copy(out=mo[:, :, 1], in_=mk_ps[:, 0:NT])
                 nc.vector.tensor_scalar(out=mo[:, :, 0], in0=mk_ps[:, 0:NT], scalar1=-1.0, scalar2=1.0,
                                         op0=ALU.mult, op1=ALU.add)
-            if 1 <= i <= NT:
-                weights(i - 1)
-            if i >= LAG:
-                back(i - LAG)
+            if i in weights_at:
+                f, n = weights_at[i]
+                nc.vector.tensor_tensor(out=w_t[:, f:f + n, 0:2], in0=mo[:, f:f + n, :],
+                                        in1=rn[:, f:f + n].unsqueeze(2).to_broadcast([P, n, 2]), op=ALU.mult)
+            for j in back_at.get(i, []):
+                back(j)
 
         for b in range(B):
             nc.vector.tensor_copy(

@@ -1,8 +1,6 @@
 from contextlib import ExitStack
 
-import concourse.bass as bass
 import concourse.mybir as mybir
-import concourse.tile as tile
 from concourse.masks import make_identity
 
 F32 = mybir.dt.float32
@@ -12,7 +10,6 @@ U8 = mybir.dt.uint8
 FP8X4 = mybir.dt.float8_e4m3fn_x4
 ALU = mybir.AluOpType
 ACT = mybir.ActivationFunctionType
-AX = mybir.AxisListType
 
 P = 128
 PACK = 4
@@ -20,16 +17,20 @@ B = 2
 C = 512
 T = 4096
 NT = B * T // P
-GROUPS = [4] * 15 + [2, 1, 1]
-PROD_BUFS = 12
-NW = 64
+TPI = NT // B
+NW = 32
+PIECE = 256
 FLOPS = 2 * B * T * C * (2 * C)
 
 CHUNKS = [(0, 0, 256), (0, 256, 256), (0, 512, 512), (0, 1024, 1024), (0, 2048, 1024), (0, 3072, 1024),
           (1, 0, 1024), (1, 1024, 1024), (1, 2048, 1024), (1, 3072, 1024)]
+GROUPS = [4] * 14 + [2, 2, 2, 1, 1]
+OFFSETS = {4: (1, 4, 6), 2: (1, 3, 5), 1: (1, 3, 5)}
+PROD_BUFS = 13
 
 
-PIECE = 256
+def scalar_takes_v(i):
+    return 10 <= i < 60 and i % 3 == 1
 
 
 def tile_hydraattention_pa_t_kernel(tc, x, mask, W_kv, b_kv, out_0, out_1):
@@ -63,6 +64,7 @@ def tile_hydraattention_pa_t_kernel(tc, x, mask, W_kv, b_kv, out_0, out_1):
         nc.vector.memset(mk_raw[:], 0.0)
         nc.scalar.dma_start(out=mk_raw[0:NT, :],
                             in_=mask.rearrange("b o (i h) w -> (b o i) (h w)", h=2))
+        nc.scalar.dma_start(out=mk_raw[NT:NT + 4, :], in_=b_kv[C:2 * C].rearrange("(q p) -> q p", p=P))
 
         warm = const.tile([P, 1], F32)
         nc.vector.memset(warm[:], 1.0)
@@ -71,6 +73,8 @@ def tile_hydraattention_pa_t_kernel(tc, x, mask, W_kv, b_kv, out_0, out_1):
         make_identity(nc, ident[:])
         res = const.tile([P, P], F32)
         nc.vector.memset(res[:], 0.0)
+        w_t = const.tile([P, NT, NW], F32)
+        nc.gpsimd.memset(w_t[:], 0.0)
 
         w_grp = const.tile([P, 2 * C, PACK], BF16, align_bytes=64)
         w_codes = const.tile([P, 2 * C], U32, align_bytes=64)
@@ -79,14 +83,14 @@ def tile_hydraattention_pa_t_kernel(tc, x, mask, W_kv, b_kv, out_0, out_1):
         x_scales = const.tile([P, B * T], U8, align_bytes=64)
         grps = {}
 
+        def regroup(engine_copy, dst, src):
+            engine_copy(out=dst.rearrange("p (c i) t -> p c t i", i=4),
+                        in_=src.rearrange("p t (c i) -> p c t i", i=4))
+
         def regroup_piece(ci, s):
-            b, c0, wc = CHUNKS[ci]
             if s == 0:
                 grps[ci] = stage.tile([P, 1024, PACK], BF16, align_bytes=64, tag="grp", name="grp")
-            grp = grps[ci]
-            nc.scalar.copy(
-                out=grp[:, s:s + PIECE, :].rearrange("p (c i) t -> p c t i", i=4),
-                in_=x_raw[ci][:, :, s:s + PIECE].rearrange("p t (c i) -> p c t i", i=4))
+            regroup(nc.scalar.copy, grps[ci][:, s:s + PIECE, :], x_raw[ci][:, :, s:s + PIECE])
 
         def quantise_chunk(ci):
             b, c0, wc = CHUNKS[ci]
@@ -96,124 +100,124 @@ def tile_hydraattention_pa_t_kernel(tc, x, mask, W_kv, b_kv, out_0, out_1):
                 scales=x_scales[:, g0:g0 + wc],
                 in_=grps[ci][:, 0:wc, :].rearrange("p w j -> p (w j)"))
 
-        regroup_piece(0, 0)
-        nc.vector.tensor_copy(
-            out=w_grp[:, 0:C, :].rearrange("p (c i) t -> p c t i", i=4),
-            in_=w_raw[0][:].rearrange("p t (c i) -> p c t i", i=4))
-        nc.scalar.copy(
-            out=w_grp[:, C:2 * C, :].rearrange("p (c i) t -> p c t i", i=4),
-            in_=w_raw[1][:].rearrange("p t (c i) -> p c t i", i=4))
-        regroup_piece(1, 0)
-        quantise_chunk(0)
-        for h in range(2):
+        def quantise_w(h):
             nc.vector.quantize_mx(
                 out=w_codes[:, h * C:(h + 1) * C].bitcast(FP8X4),
                 scales=w_scales[:, h * C:(h + 1) * C],
                 in_=w_grp[:, h * C:(h + 1) * C, :].rearrange("p w j -> p (w j)"))
-        quantise_chunk(1)
+
+        regroup_piece(0, 0)
+        regroup(nc.vector.tensor_copy, w_grp[:, 0:C, :], w_raw[0][:])
+        regroup(nc.scalar.copy, w_grp[:, C:C + 256, :], w_raw[1][:, :, 0:256])
+        quantise_chunk(0)
+        regroup(nc.vector.tensor_copy, w_grp[:, C + 256:2 * C, :], w_raw[1][:, :, 256:C])
+        quantise_w(0)
+        regroup_piece(1, 0)
+        quantise_w(1)
 
         piece_at = {}
-        quant_at = {}
+        quant_at = {0: 1}
+        free_step = 0
         for ci in range(2, len(CHUNKS)):
             b, c0, wc = CHUNKS[ci]
-            first = (b * T + c0) // P
-            n_pieces = wc // PIECE
-            begin = 0 if ci == 2 else (2 if ci == 3 else first - 8)
-            for k in range(n_pieces):
-                piece_at[begin + k] = (ci, k * PIECE)
-            quant_at[begin + n_pieces + (0 if ci <= 3 else 2)] = ci
-
-        mk_f = const.tile([P, P], F32)
-        mo = const.tile([P, NT, 2], F32)
-        n2 = const.tile([P, NT], F32)
-        nrm = const.tile([P, NT], F32)
-        rn = const.tile([P, NT], F32)
-        w_t = const.tile([P, NT, NW], F32)
-        nc.gpsimd.memset(w_t[:], 0.0)
-        reds = [psum1.tile([P, 4, NW], F32, tag="red0", name="red0"), psum1.tile([P, 4, NW], F32, tag="red1", name="red1")]
-        prods = {}
-
-        def back(i):
-            p_sb = prods[i]
-            b = i // (NT // B)
-            ib = i % (NT // B)
-            for q in range(4):
-                nc.tensor.matmul(out=reds[b][:, q, :], lhsT=p_sb[:, q * P:(q + 1) * P],
-                                 rhs=w_t[:, i, :], start=(ib == 0 and q == 0),
-                                 stop=(ib == NT // B - 1 and q == 3))
-
+            begin = max(free_step, (b * T + c0) // P - 10)
+            steps = [s for s in range(begin, begin + 8) if not scalar_takes_v(s)][0:wc // PIECE]
+            for k, s in enumerate(steps):
+                piece_at[s] = (ci, k * PIECE)
+            free_step = steps[-1] + 1
+            quant_at[free_step + (0 if ci <= 3 else 1)] = ci
         sqrt_at = {}
         weights_at = {}
         back_at = {}
         first = 0
         for n in GROUPS:
             last = first + n - 1
-            sqrt_at[last + 1] = (first, n)
-            weights_at[last + 3] = (first, n)
+            o_sqrt, o_weights, o_back = OFFSETS[n]
+            sqrt_at[last + o_sqrt] = sqrt_at.get(last + o_sqrt, []) + [(first, n)]
+            weights_at[last + o_weights] = weights_at.get(last + o_weights, []) + [(first, n)]
             for k in range(n):
-                back_at[last + 5 + k] = back_at.get(last + 5 + k, []) + [first + k]
+                back_at[last + o_back + k] = back_at.get(last + o_back + k, []) + [first + k]
             first += n
         n_steps = max(back_at) + 1
+        order = [j for i in range(n_steps) for j in back_at.get(i, [])]
+        first_of_image = [[j for j in order if j // TPI == b][0] for b in range(B)]
+        last_of_image = [[j for j in order if j // TPI == b][-1] for b in range(B)]
 
-        def front_k(i):
-            t0 = i * P
-            kps = psum.tile([P, C], F32, tag="kps")
-            vps = psum.tile([P, C], F32, tag="vps")
-            for h, acc in ((0, kps), (1, vps)):
-                nc.tensor.matmul_mx(
-                    out=acc[:],
-                    lhsT=x_codes[:, t0:t0 + P].bitcast(FP8X4),
-                    lhsT_scale=x_scales[:, t0:t0 + P],
-                    rhs=w_codes[:, h * C:(h + 1) * C].bitcast(FP8X4),
-                    rhs_scale=w_scales[:, h * C:(h + 1) * C],
-                    start=True, stop=True)
-            k_sb = work.tile([P, C], F32, tag="k_sb")
-            nc.vector.tensor_tensor(out=k_sb[:], in0=kps[:], in1=bias_b[:, 0:C], op=ALU.add)
-            junk = work.tile([P, C], BF16, tag="junk")
-            nc.scalar.activation(out=junk[:], in_=k_sb[:], func=ACT.Square, accum_out=n2[:, i:i + 1])
-            return k_sb, vps
+        mk_f = const.tile([P, P], F32)
+        mo = const.tile([P, NT, 2], F32)
+        bv_t = const.tile([P, 4], F32)
+        corr = const.tile([P, B, 4, 2], F32)
+        n2 = const.tile([P, NT], F32)
+        nrm = const.tile([P, NT], F32)
+        rn = const.tile([P, NT], F32)
+        reds = [psum1.tile([P, 8, NW], F32, tag="red%d" % b, name="red%d" % b) for b in range(B)]
+        held = {}
 
-        def front_v(i, k_sb, vps):
-            v_sb = work.tile([P, C], F32, tag="v_sb")
-            nc.vector.tensor_tensor(out=v_sb[:], in0=vps[:], in1=bias_b[:, C:2 * C], op=ALU.add)
-            p_sb = prod.tile([P, C], F32, tag="p_sb")
-            nc.gpsimd.tensor_tensor(out=p_sb[:], in0=k_sb[:], in1=v_sb[:], op=ALU.mult)
-            prods[i] = p_sb
+        def back(j):
+            b = j // TPI
+            n_q = 8 if scalar_takes_v(j) else 4
+            for q in range(n_q):
+                nc.tensor.matmul(out=reds[b][:, q, :], lhsT=held[j][q // 4][:, (q % 4) * P:(q % 4 + 1) * P],
+                                 rhs=w_t[:, j, :], start=(j == first_of_image[b] and q == 0),
+                                 stop=(j == last_of_image[b] and q == n_q - 1))
 
         for i in range(n_steps):
-            if i == 0:
-                nc.vector.tensor_copy(out=mk_f[:], in_=mk_raw[:])
-                mk_ps = psum.tile([P, C], F32, tag="kps", name="mk_ps")
-                nc.tensor.transpose(mk_ps[:, 0:P], mk_f[:], ident[:])
             if i < NT:
-                k_sb, vps = front_k(i)
-            if i in weights_at:
-                f, n = weights_at[i]
+                t0 = i * P
+                kps = psum.tile([P, C], F32, tag="kps")
+                vps = psum.tile([P, C], F32, tag="vps")
+                for h, acc in ((0, kps), (1, vps)):
+                    nc.tensor.matmul_mx(
+                        out=acc[:],
+                        lhsT=x_codes[:, t0:t0 + P].bitcast(FP8X4),
+                        lhsT_scale=x_scales[:, t0:t0 + P],
+                        rhs=w_codes[:, h * C:(h + 1) * C].bitcast(FP8X4),
+                        rhs_scale=w_scales[:, h * C:(h + 1) * C],
+                        start=True, stop=True)
+                k_sb = prod.tile([P, C], F32, tag="k_sb")
+                nc.vector.tensor_tensor(out=k_sb[:], in0=kps[:], in1=bias_b[:, 0:C], op=ALU.add)
+                v_sb = work.tile([P, C], F32, tag="v_sb")
+                if scalar_takes_v(i):
+                    nc.scalar.copy(out=v_sb[:], in_=vps[:])
+                junk = work.tile([P, C], BF16, tag="junk")
+                nc.scalar.activation(out=junk[:], in_=k_sb[:], func=ACT.Square, accum_out=n2[:, i:i + 1])
+            for f, n in weights_at.get(i, []):
                 nc.vector.reciprocal(out=rn[:, f:f + n], in_=nrm[:, f:f + n])
             if i < NT:
-                front_v(i, k_sb, vps)
-            if i in sqrt_at:
-                f, n = sqrt_at[i]
+                if not scalar_takes_v(i):
+                    nc.vector.tensor_tensor(out=v_sb[:], in0=vps[:], in1=bias_b[:, C:2 * C], op=ALU.add)
+                p_sb = prod.tile([P, C], F32, tag="p_sb")
+                nc.gpsimd.tensor_tensor(out=p_sb[:], in0=k_sb[:], in1=v_sb[:], op=ALU.mult)
+                held[i] = (p_sb, k_sb)
+            for f, n in sqrt_at.get(i, []):
                 nc.scalar.activation(out=nrm[:, f:f + n], in_=n2[:, f:f + n], func=ACT.Sqrt)
             if i in piece_at:
                 regroup_piece(piece_at[i][0], piece_at[i][1])
             if i in quant_at:
                 quantise_chunk(quant_at[i])
-            if i == 0:
+            if i == 1:
+                nc.vector.tensor_copy(out=mk_f[:], in_=mk_raw[:])
+            if i == 2:
+                mk_ps = psum.tile([P, C], F32, tag="kps", name="mk_ps")
+                nc.tensor.transpose(mk_ps[:, 0:P], mk_f[:], ident[:])
+            if i == 3:
+                nc.vector.tensor_copy(out=bv_t[:], in_=mk_ps[:, NT:NT + 4])
                 nc.vector.tensor_copy(out=mo[:, :, 1], in_=mk_ps[:, 0:NT])
                 nc.vector.tensor_scalar(out=mo[:, :, 0], in0=mk_ps[:, 0:NT], scalar1=-1.0, scalar2=1.0,
                                         op0=ALU.mult, op1=ALU.add)
-            if i in weights_at:
-                f, n = weights_at[i]
+            for f, n in weights_at.get(i, []):
                 nc.vector.tensor_tensor(out=w_t[:, f:f + n, 0:2], in0=mo[:, f:f + n, :],
                                         in1=rn[:, f:f + n].unsqueeze(2).to_broadcast([P, n, 2]), op=ALU.mult)
             for j in back_at.get(i, []):
                 back(j)
 
         for b in range(B):
-            nc.vector.tensor_copy(
+            nc.vector.tensor_tensor(out=corr[:, b, :, :], in0=reds[b][:, 4:8, 0:2],
+                                    in1=bv_t[:].unsqueeze(2).to_broadcast([P, 4, 2]), op=ALU.mult)
+            nc.vector.tensor_tensor(
                 out=res[:, 0:16].rearrange("p (j b q) -> p j b q", j=2, b=B)[:, :, b, :],
-                in_=reds[b][:, :, 0:2].rearrange("p q j -> p j q"))
+                in0=reds[b][:, 0:4, 0:2].rearrange("p q j -> p j q"),
+                in1=corr[:, b, :, :].rearrange("p q j -> p j q"), op=ALU.add)
         res_ps = psum.tile([P, C], F32, tag="kps", name="res_ps")
         nc.tensor.transpose(res_ps[:, 0:P], res[:], ident[:])
         res_t = const.tile([16, P], F32)

@@ -10,6 +10,7 @@ U8 = mybir.dt.uint8
 FP8X4 = mybir.dt.float8_e4m3fn_x4
 ALU = mybir.AluOpType
 ACT = mybir.ActivationFunctionType
+AX = mybir.AxisListType
 
 P = 128
 PACK = 4
@@ -18,7 +19,7 @@ C = 512
 T = 4096
 NT = B * T // P
 TPI = NT // B
-NW = 32
+NW = 64
 PIECE = 256
 FLOPS = 2 * B * T * C * (2 * C)
 
@@ -29,8 +30,8 @@ OFFSETS = {4: (1, 4, 6), 2: (1, 3, 5), 1: (1, 3, 5)}
 PROD_BUFS = 13
 
 
-def scalar_takes_v(i):
-    return 10 <= i < 60 and i % 3 == 1
+def by_transposes(j):
+    return j % 2 == 1 and j % TPI < 26
 
 
 def tile_hydraattention_pa_t_kernel(tc, x, mask, W_kv, b_kv, out_0, out_1):
@@ -40,7 +41,9 @@ def tile_hydraattention_pa_t_kernel(tc, x, mask, W_kv, b_kv, out_0, out_1):
         stage = ctx.enter_context(tc.tile_pool(name="stage", bufs=2))
         work = ctx.enter_context(tc.tile_pool(name="work", bufs=4))
         prod = ctx.enter_context(tc.tile_pool(name="prod", bufs=PROD_BUFS))
-        psum = ctx.enter_context(tc.psum_pool(name="psum", bufs=3))
+        psum_k = ctx.enter_context(tc.psum_pool(name="psum_k", bufs=2))
+        psum_v = ctx.enter_context(tc.psum_pool(name="psum_v", bufs=3))
+        scaled = ctx.enter_context(tc.tile_pool(name="scaled", bufs=3))
         psum1 = ctx.enter_context(tc.psum_pool(name="psum1", bufs=1))
         ctx.enter_context(tc.manual_schedule())
 
@@ -64,7 +67,6 @@ def tile_hydraattention_pa_t_kernel(tc, x, mask, W_kv, b_kv, out_0, out_1):
         nc.vector.memset(mk_raw[:], 0.0)
         nc.scalar.dma_start(out=mk_raw[0:NT, :],
                             in_=mask.rearrange("b o (i h) w -> (b o i) (h w)", h=2))
-        nc.scalar.dma_start(out=mk_raw[NT:NT + 4, :], in_=b_kv[C:2 * C].rearrange("(q p) -> q p", p=P))
 
         warm = const.tile([P, 1], F32)
         nc.vector.memset(warm[:], 1.0)
@@ -121,13 +123,14 @@ def tile_hydraattention_pa_t_kernel(tc, x, mask, W_kv, b_kv, out_0, out_1):
         for ci in range(2, len(CHUNKS)):
             b, c0, wc = CHUNKS[ci]
             begin = max(free_step, (b * T + c0) // P - 10)
-            steps = [s for s in range(begin, begin + 8) if not scalar_takes_v(s)][0:wc // PIECE]
+            steps = [s for s in range(begin, begin + 8)][0:wc // PIECE]
             for k, s in enumerate(steps):
                 piece_at[s] = (ci, k * PIECE)
             free_step = steps[-1] + 1
             quant_at[free_step + (0 if ci <= 3 else 1)] = ci
         sqrt_at = {}
         weights_at = {}
+        scale_at = {}
         back_at = {}
         first = 0
         for n in GROUPS:
@@ -136,36 +139,60 @@ def tile_hydraattention_pa_t_kernel(tc, x, mask, W_kv, b_kv, out_0, out_1):
             sqrt_at[last + o_sqrt] = sqrt_at.get(last + o_sqrt, []) + [(first, n)]
             weights_at[last + o_weights] = weights_at.get(last + o_weights, []) + [(first, n)]
             for k in range(n):
-                back_at[last + o_back + k] = back_at.get(last + o_back + k, []) + [first + k]
+                if by_transposes(first + k):
+                    scale_at[last + o_back + k - 1] = scale_at.get(last + o_back + k - 1, []) + [first + k]
+                    back_at[last + o_back + k + 1] = back_at.get(last + o_back + k + 1, []) + [first + k]
+                else:
+                    back_at[last + o_back + k] = back_at.get(last + o_back + k, []) + [first + k]
             first += n
         n_steps = max(back_at) + 1
         order = [j for i in range(n_steps) for j in back_at.get(i, [])]
-        first_of_image = [[j for j in order if j // TPI == b][0] for b in range(B)]
-        last_of_image = [[j for j in order if j // TPI == b][-1] for b in range(B)]
+        first_m = [[j for j in order if j // TPI == b and not by_transposes(j)][0] for b in range(B)]
+        last_m = [[j for j in order if j // TPI == b and not by_transposes(j)][-1] for b in range(B)]
+        first_t = [[j for j in order if j // TPI == b and by_transposes(j)][0] for b in range(B)]
+        last_t = [[j for j in order if j // TPI == b and by_transposes(j)][-1] for b in range(B)]
 
         mk_f = const.tile([P, P], F32)
         mo = const.tile([P, NT, 2], F32)
-        bv_t = const.tile([P, 4], F32)
-        corr = const.tile([P, B, 4, 2], F32)
+        acc_sum = const.tile([P, 2, B, 4], F32)
         n2 = const.tile([P, NT], F32)
         nrm = const.tile([P, NT], F32)
         rn = const.tile([P, NT], F32)
-        reds = [psum1.tile([P, 8, NW], F32, tag="red%d" % b, name="red%d" % b) for b in range(B)]
+        red = psum1.tile([P, B, 4, NW], F32, tag="red")
+        accs = [psum1.tile([P, 4, P], F32, tag="acc%d" % w, name="acc%d" % w) for w in range(2)]
         held = {}
+        weighted = {}
+
+        def scale(j):
+            p_know = scaled.tile([P, C], F32, tag="p_know")
+            nc.scalar.activation(out=p_know[:], in_=held[j][:], func=ACT.Copy, scale=w_t[:, j, 0:1])
+            p_mask = scaled.tile([P, C], F32, tag="p_mask")
+            nc.gpsimd.tensor_scalar(out=p_mask[:], in0=held[j][:], scalar1=w_t[:, j, 1:2], scalar2=0.0,
+                                    op0=ALU.mult, op1=ALU.add)
+            weighted[j] = (p_know, p_mask)
 
         def back(j):
             b = j // TPI
-            n_q = 8 if scalar_takes_v(j) else 4
-            for q in range(n_q):
-                nc.tensor.matmul(out=reds[b][:, q, :], lhsT=held[j][q // 4][:, (q % 4) * P:(q % 4 + 1) * P],
-                                 rhs=w_t[:, j, :], start=(j == first_of_image[b] and q == 0),
-                                 stop=(j == last_of_image[b] and q == n_q - 1))
+            if by_transposes(j):
+                for w in range(2):
+                    for q in range(4):
+                        nc.tensor.matmul(out=accs[w][:, q, :], lhsT=weighted[j][w][:, q * P:(q + 1) * P],
+                                         rhs=ident[:], is_transpose=True,
+                                         start=(j == first_t[b] and q == 0), stop=(j == last_t[b] and q == 3))
+                if j == last_t[b]:
+                    for w in range(2):
+                        nc.vector.tensor_reduce(out=acc_sum[:, w, b, :], in_=accs[w][:], axis=AX.X, op=ALU.add)
+            else:
+                for q in range(4):
+                    nc.tensor.matmul(out=red[:, b, q, :], lhsT=held[j][:, q * P:(q + 1) * P],
+                                     rhs=w_t[:, j, :], start=(j == first_m[b] and q == 0),
+                                     stop=(j == last_m[b] and q == 3))
 
         for i in range(n_steps):
             if i < NT:
                 t0 = i * P
-                kps = psum.tile([P, C], F32, tag="kps")
-                vps = psum.tile([P, C], F32, tag="vps")
+                kps = psum_k.tile([P, C], F32, tag="kps")
+                vps = psum_v.tile([P, C], F32, tag="vps")
                 for h, acc in ((0, kps), (1, vps)):
                     nc.tensor.matmul_mx(
                         out=acc[:],
@@ -174,23 +201,22 @@ def tile_hydraattention_pa_t_kernel(tc, x, mask, W_kv, b_kv, out_0, out_1):
                         rhs=w_codes[:, h * C:(h + 1) * C].bitcast(FP8X4),
                         rhs_scale=w_scales[:, h * C:(h + 1) * C],
                         start=True, stop=True)
-                k_sb = prod.tile([P, C], F32, tag="k_sb")
+                k_sb = work.tile([P, C], F32, tag="k_sb")
                 nc.vector.tensor_tensor(out=k_sb[:], in0=kps[:], in1=bias_b[:, 0:C], op=ALU.add)
                 v_sb = work.tile([P, C], F32, tag="v_sb")
-                if scalar_takes_v(i):
-                    nc.scalar.copy(out=v_sb[:], in_=vps[:])
                 junk = work.tile([P, C], BF16, tag="junk")
                 nc.scalar.activation(out=junk[:], in_=k_sb[:], func=ACT.Square, accum_out=n2[:, i:i + 1])
             for f, n in weights_at.get(i, []):
                 nc.vector.reciprocal(out=rn[:, f:f + n], in_=nrm[:, f:f + n])
             if i < NT:
-                if not scalar_takes_v(i):
-                    nc.vector.tensor_tensor(out=v_sb[:], in0=vps[:], in1=bias_b[:, C:2 * C], op=ALU.add)
+                nc.vector.tensor_tensor(out=v_sb[:], in0=vps[:], in1=bias_b[:, C:2 * C], op=ALU.add)
                 p_sb = prod.tile([P, C], F32, tag="p_sb")
                 nc.gpsimd.tensor_tensor(out=p_sb[:], in0=k_sb[:], in1=v_sb[:], op=ALU.mult)
-                held[i] = (p_sb, k_sb)
+                held[i] = p_sb
             for f, n in sqrt_at.get(i, []):
                 nc.scalar.activation(out=nrm[:, f:f + n], in_=n2[:, f:f + n], func=ACT.Sqrt)
+            for j in scale_at.get(i, []):
+                scale(j)
             if i in piece_at:
                 regroup_piece(piece_at[i][0], piece_at[i][1])
             if i in quant_at:
@@ -198,10 +224,9 @@ def tile_hydraattention_pa_t_kernel(tc, x, mask, W_kv, b_kv, out_0, out_1):
             if i == 1:
                 nc.vector.tensor_copy(out=mk_f[:], in_=mk_raw[:])
             if i == 2:
-                mk_ps = psum.tile([P, C], F32, tag="kps", name="mk_ps")
+                mk_ps = psum_k.tile([P, C], F32, tag="kps", name="mk_ps")
                 nc.tensor.transpose(mk_ps[:, 0:P], mk_f[:], ident[:])
             if i == 3:
-                nc.vector.tensor_copy(out=bv_t[:], in_=mk_ps[:, NT:NT + 4])
                 nc.vector.tensor_copy(out=mo[:, :, 1], in_=mk_ps[:, 0:NT])
                 nc.vector.tensor_scalar(out=mo[:, :, 0], in0=mk_ps[:, 0:NT], scalar1=-1.0, scalar2=1.0,
                                         op0=ALU.mult, op1=ALU.add)
@@ -212,13 +237,11 @@ def tile_hydraattention_pa_t_kernel(tc, x, mask, W_kv, b_kv, out_0, out_1):
                 back(j)
 
         for b in range(B):
-            nc.vector.tensor_tensor(out=corr[:, b, :, :], in0=reds[b][:, 4:8, 0:2],
-                                    in1=bv_t[:].unsqueeze(2).to_broadcast([P, 4, 2]), op=ALU.mult)
             nc.vector.tensor_tensor(
                 out=res[:, 0:16].rearrange("p (j b q) -> p j b q", j=2, b=B)[:, :, b, :],
-                in0=reds[b][:, 0:4, 0:2].rearrange("p q j -> p j q"),
-                in1=corr[:, b, :, :].rearrange("p q j -> p j q"), op=ALU.add)
-        res_ps = psum.tile([P, C], F32, tag="kps", name="res_ps")
+                in0=red[:, b, :, 0:2].rearrange("p q j -> p j q"),
+                in1=acc_sum[:, :, b, :], op=ALU.add)
+        res_ps = psum_k.tile([P, C], F32, tag="kps", name="res_ps")
         nc.tensor.transpose(res_ps[:, 0:P], res[:], ident[:])
         res_t = const.tile([16, P], F32)
         nc.scalar.copy(out=res_t[:], in_=res_ps[0:16, 0:P])

@@ -10,28 +10,28 @@ U8 = mybir.dt.uint8
 FP8X4 = mybir.dt.float8_e4m3fn_x4
 ALU = mybir.AluOpType
 ACT = mybir.ActivationFunctionType
-AX = mybir.AxisListType
 
 P = 128
 PACK = 4
 B = 2
 C = 512
 T = 4096
-NT = B * T // P
-TPI = NT // B
-NW = 64
-PIECE = 256
+N_TILES = B * T // P
+TILES_PER_IMAGE = T // P
+C_BLOCKS = C // P
 FLOPS = 2 * B * T * C * (2 * C)
+
+POOL_COLS = 64
 
 CHUNKS = [(0, 0, 256), (0, 256, 256), (0, 512, 512), (0, 1024, 1024), (0, 2048, 1024), (0, 3072, 1024),
           (1, 0, 1024), (1, 1024, 1024), (1, 2048, 1024), (1, 3072, 1024)]
+MAX_CHUNK = 1024
+PIECE = 256
+CHUNK_LEAD = 10
+
 GROUPS = [4] * 14 + [2, 2, 2, 1, 1]
-OFFSETS = {4: (1, 4, 6), 2: (1, 3, 5), 1: (1, 3, 5)}
-PROD_BUFS = 13
-
-
-def by_transposes(j):
-    return j % 2 == 1 and j % TPI < 26
+DISTANCES = {4: (1, 4, 6), 2: (1, 3, 5), 1: (1, 3, 5)}
+PRODUCT_BUFS = 7
 
 
 def tile_hydraattention_pa_t_kernel(tc, x, mask, W_kv, b_kv, out_0, out_1):
@@ -39,33 +39,36 @@ def tile_hydraattention_pa_t_kernel(tc, x, mask, W_kv, b_kv, out_0, out_1):
     with ExitStack() as ctx:
         const = ctx.enter_context(tc.tile_pool(name="const", bufs=1))
         stage = ctx.enter_context(tc.tile_pool(name="stage", bufs=2))
-        work = ctx.enter_context(tc.tile_pool(name="work", bufs=4))
-        prod = ctx.enter_context(tc.tile_pool(name="prod", bufs=PROD_BUFS))
-        psum_k = ctx.enter_context(tc.psum_pool(name="psum_k", bufs=2))
-        psum_v = ctx.enter_context(tc.psum_pool(name="psum_v", bufs=3))
-        scaled = ctx.enter_context(tc.tile_pool(name="scaled", bufs=3))
-        psum1 = ctx.enter_context(tc.psum_pool(name="psum1", bufs=1))
+        work = ctx.enter_context(tc.tile_pool(name="work", bufs=3))
+        products = ctx.enter_context(tc.tile_pool(name="products", bufs=PRODUCT_BUFS))
+        psum_k = ctx.enter_context(tc.psum_pool(name="psum_k", bufs=3))
+        psum_v = ctx.enter_context(tc.psum_pool(name="psum_v", bufs=4))
+        psum_pool = ctx.enter_context(tc.psum_pool(name="psum_pool", bufs=1))
         ctx.enter_context(tc.manual_schedule())
 
         w_raw = [const.tile([P, PACK, C], BF16, name="w_raw%d" % h) for h in range(2)]
-        x_raw = [const.tile([P, PACK, wc], BF16, name="x_raw%d" % ci) for ci, (b, c0, wc) in enumerate(CHUNKS)]
+        x_raw = [const.tile([P, PACK, width], BF16, name="x_raw%d" % ci)
+                 for ci, (b, p0, width) in enumerate(CHUNKS)]
 
-        def load_x(ci):
-            b, c0, wc = CHUNKS[ci]
-            nc.sync.dma_start(out=x_raw[ci][:],
-                              in_=x[b].rearrange("(p j) h w -> p j (h w)", j=PACK)[:, :, c0:c0 + wc])
-
-        load_x(0)
-        for h in range(2):
+        def load_w(h):
             nc.sync.dma_start(out=w_raw[h][:],
                               in_=W_kv.rearrange("(p j) n -> p j n", j=PACK)[:, :, h * C:(h + 1) * C])
+
+        def load_x(ci):
+            b, p0, width = CHUNKS[ci]
+            nc.sync.dma_start(out=x_raw[ci][:],
+                              in_=x[b].rearrange("(p j) h w -> p j (h w)", j=PACK)[:, :, p0:p0 + width])
+
+        load_w(0)
+        load_x(0)
+        load_w(1)
         for ci in range(1, len(CHUNKS)):
             load_x(ci)
-        bias_b = const.tile([P, 2 * C], BF16)
-        nc.scalar.dma_start(out=bias_b[:], in_=b_kv.partition_broadcast(P))
-        mk_raw = const.tile([P, P], BF16)
-        nc.vector.memset(mk_raw[:], 0.0)
-        nc.scalar.dma_start(out=mk_raw[0:NT, :],
+        bias_rows = const.tile([P, 2 * C], BF16)
+        nc.scalar.dma_start(out=bias_rows[:], in_=b_kv.partition_broadcast(P))
+        mask_rows = const.tile([P, P], BF16)
+        nc.vector.memset(mask_rows[:], 0.0)
+        nc.scalar.dma_start(out=mask_rows[0:N_TILES, :],
                             in_=mask.rearrange("b o (i h) w -> (b o i) (h w)", h=2))
 
         warm = const.tile([P, 1], F32)
@@ -73,177 +76,145 @@ def tile_hydraattention_pa_t_kernel(tc, x, mask, W_kv, b_kv, out_0, out_1):
         nc.scalar.activation(out=warm[:], in_=warm[:], func=ACT.Sqrt)
         ident = const.tile([P, P], F32)
         make_identity(nc, ident[:])
-        res = const.tile([P, P], F32)
-        nc.vector.memset(res[:], 0.0)
-        w_t = const.tile([P, NT, NW], F32)
-        nc.gpsimd.memset(w_t[:], 0.0)
+        result = const.tile([P, P], F32)
+        nc.vector.memset(result[:], 0.0)
+        weights = const.tile([P, N_TILES, POOL_COLS], F32)
+        nc.gpsimd.memset(weights[:], 0.0)
 
-        w_grp = const.tile([P, 2 * C, PACK], BF16, align_bytes=64)
+        w_grouped = const.tile([P, 2 * C, PACK], BF16, align_bytes=64)
         w_codes = const.tile([P, 2 * C], U32, align_bytes=64)
         w_scales = const.tile([P, 2 * C], U8, align_bytes=64)
         x_codes = const.tile([P, B * T], U32, align_bytes=64)
         x_scales = const.tile([P, B * T], U8, align_bytes=64)
-        grps = {}
+        x_grouped = {}
 
-        def regroup(engine_copy, dst, src):
-            engine_copy(out=dst.rearrange("p (c i) t -> p c t i", i=4),
-                        in_=src.rearrange("p t (c i) -> p c t i", i=4))
+        def regroup(copy, dst, src):
+            copy(out=dst.rearrange("p (c i) j -> p c j i", i=4), in_=src.rearrange("p j (c i) -> p c j i", i=4))
 
-        def regroup_piece(ci, s):
-            if s == 0:
-                grps[ci] = stage.tile([P, 1024, PACK], BF16, align_bytes=64, tag="grp", name="grp")
-            regroup(nc.scalar.copy, grps[ci][:, s:s + PIECE, :], x_raw[ci][:, :, s:s + PIECE])
+        def regroup_piece(ci, first_pixel):
+            if first_pixel == 0:
+                x_grouped[ci] = stage.tile([P, MAX_CHUNK, PACK], BF16, align_bytes=64, tag="x_grouped",
+                                           name="x_grouped")
+            cols = slice(first_pixel, first_pixel + PIECE)
+            regroup(nc.scalar.copy, x_grouped[ci][:, cols, :], x_raw[ci][:, :, cols])
 
         def quantise_chunk(ci):
-            b, c0, wc = CHUNKS[ci]
-            g0 = b * T + c0
-            nc.vector.quantize_mx(
-                out=x_codes[:, g0:g0 + wc].bitcast(FP8X4),
-                scales=x_scales[:, g0:g0 + wc],
-                in_=grps[ci][:, 0:wc, :].rearrange("p w j -> p (w j)"))
+            b, p0, width = CHUNKS[ci]
+            cols = slice(b * T + p0, b * T + p0 + width)
+            nc.vector.quantize_mx(out=x_codes[:, cols].bitcast(FP8X4), scales=x_scales[:, cols],
+                                  in_=x_grouped[ci][:, 0:width, :].rearrange("p w j -> p (w j)"))
 
         def quantise_w(h):
-            nc.vector.quantize_mx(
-                out=w_codes[:, h * C:(h + 1) * C].bitcast(FP8X4),
-                scales=w_scales[:, h * C:(h + 1) * C],
-                in_=w_grp[:, h * C:(h + 1) * C, :].rearrange("p w j -> p (w j)"))
+            cols = slice(h * C, (h + 1) * C)
+            nc.vector.quantize_mx(out=w_codes[:, cols].bitcast(FP8X4), scales=w_scales[:, cols],
+                                  in_=w_grouped[:, cols, :].rearrange("p w j -> p (w j)"))
 
+        regroup(nc.vector.tensor_copy, w_grouped[:, 0:C, :], w_raw[0][:])
         regroup_piece(0, 0)
-        regroup(nc.vector.tensor_copy, w_grp[:, 0:C, :], w_raw[0][:])
-        regroup(nc.scalar.copy, w_grp[:, C:C + 256, :], w_raw[1][:, :, 0:256])
-        quantise_chunk(0)
-        regroup(nc.vector.tensor_copy, w_grp[:, C + 256:2 * C, :], w_raw[1][:, :, 256:C])
+        regroup(nc.scalar.copy, w_grouped[:, C:C + C // 2, :], w_raw[1][:, :, 0:C // 2])
         quantise_w(0)
+        quantise_chunk(0)
+        regroup(nc.vector.tensor_copy, w_grouped[:, C + C // 2:2 * C, :], w_raw[1][:, :, C // 2:C])
         regroup_piece(1, 0)
         quantise_w(1)
 
         piece_at = {}
-        quant_at = {0: 1}
+        quantise_at = {0: 1}
         free_step = 0
         for ci in range(2, len(CHUNKS)):
-            b, c0, wc = CHUNKS[ci]
-            begin = max(free_step, (b * T + c0) // P - 10)
-            steps = [s for s in range(begin, begin + 8)][0:wc // PIECE]
-            for k, s in enumerate(steps):
-                piece_at[s] = (ci, k * PIECE)
-            free_step = steps[-1] + 1
-            quant_at[free_step + (0 if ci <= 3 else 1)] = ci
+            b, p0, width = CHUNKS[ci]
+            begin = max(free_step, (b * T + p0) // P - CHUNK_LEAD)
+            for n in range(width // PIECE):
+                piece_at[begin + n] = (ci, n * PIECE)
+            free_step = begin + width // PIECE
+            quantise_at[free_step + (0 if ci <= 3 else 1)] = ci
         sqrt_at = {}
         weights_at = {}
-        scale_at = {}
-        back_at = {}
+        pool_at = {}
         first = 0
-        for n in GROUPS:
-            last = first + n - 1
-            o_sqrt, o_weights, o_back = OFFSETS[n]
-            sqrt_at[last + o_sqrt] = sqrt_at.get(last + o_sqrt, []) + [(first, n)]
-            weights_at[last + o_weights] = weights_at.get(last + o_weights, []) + [(first, n)]
-            for k in range(n):
-                if by_transposes(first + k):
-                    scale_at[last + o_back + k - 1] = scale_at.get(last + o_back + k - 1, []) + [first + k]
-                    back_at[last + o_back + k + 1] = back_at.get(last + o_back + k + 1, []) + [first + k]
-                else:
-                    back_at[last + o_back + k] = back_at.get(last + o_back + k, []) + [first + k]
-            first += n
-        n_steps = max(back_at) + 1
-        order = [j for i in range(n_steps) for j in back_at.get(i, [])]
-        first_m = [[j for j in order if j // TPI == b and not by_transposes(j)][0] for b in range(B)]
-        last_m = [[j for j in order if j // TPI == b and not by_transposes(j)][-1] for b in range(B)]
-        first_t = [[j for j in order if j // TPI == b and by_transposes(j)][0] for b in range(B)]
-        last_t = [[j for j in order if j // TPI == b and by_transposes(j)][-1] for b in range(B)]
+        for size in GROUPS:
+            last = first + size - 1
+            d_sqrt, d_weights, d_pool = DISTANCES[size]
+            sqrt_at[last + d_sqrt] = sqrt_at.get(last + d_sqrt, []) + [(first, size)]
+            weights_at[last + d_weights] = weights_at.get(last + d_weights, []) + [(first, size)]
+            for n in range(size):
+                pool_at[last + d_pool + n] = pool_at.get(last + d_pool + n, []) + [first + n]
+            first += size
+        n_steps = max(pool_at) + 1
+        pool_order = [t for i in range(n_steps) for t in pool_at.get(i, [])]
+        opens_group = [[t for t in pool_order if t // TILES_PER_IMAGE == b][0] for b in range(B)]
+        closes_group = [[t for t in pool_order if t // TILES_PER_IMAGE == b][-1] for b in range(B)]
 
-        mk_f = const.tile([P, P], F32)
-        mo = const.tile([P, NT, 2], F32)
-        acc_sum = const.tile([P, 2, B, 4], F32)
-        n2 = const.tile([P, NT], F32)
-        nrm = const.tile([P, NT], F32)
-        rn = const.tile([P, NT], F32)
-        red = psum1.tile([P, B, 4, NW], F32, tag="red")
-        accs = [psum1.tile([P, 4, P], F32, tag="acc%d" % w, name="acc%d" % w) for w in range(2)]
-        held = {}
-        weighted = {}
+        mask_f32 = const.tile([P, P], F32)
+        mask_pair = const.tile([P, N_TILES, 2], F32)
+        norm_sq = const.tile([P, N_TILES], F32)
+        norm = const.tile([P, N_TILES], F32)
+        inv_norm = const.tile([P, N_TILES], F32)
+        pooled = psum_pool.tile([P, B, C_BLOCKS, POOL_COLS], F32)
+        product_of = {}
 
-        def scale(j):
-            p_know = scaled.tile([P, C], F32, tag="p_know")
-            nc.scalar.activation(out=p_know[:], in_=held[j][:], func=ACT.Copy, scale=w_t[:, j, 0:1])
-            p_mask = scaled.tile([P, C], F32, tag="p_mask")
-            nc.gpsimd.tensor_scalar(out=p_mask[:], in0=held[j][:], scalar1=w_t[:, j, 1:2], scalar2=0.0,
-                                    op0=ALU.mult, op1=ALU.add)
-            weighted[j] = (p_know, p_mask)
-
-        def back(j):
-            b = j // TPI
-            if by_transposes(j):
-                for w in range(2):
-                    for q in range(4):
-                        nc.tensor.matmul(out=accs[w][:, q, :], lhsT=weighted[j][w][:, q * P:(q + 1) * P],
-                                         rhs=ident[:], is_transpose=True,
-                                         start=(j == first_t[b] and q == 0), stop=(j == last_t[b] and q == 3))
-                if j == last_t[b]:
-                    for w in range(2):
-                        nc.vector.tensor_reduce(out=acc_sum[:, w, b, :], in_=accs[w][:], axis=AX.X, op=ALU.add)
-            else:
-                for q in range(4):
-                    nc.tensor.matmul(out=red[:, b, q, :], lhsT=held[j][:, q * P:(q + 1) * P],
-                                     rhs=w_t[:, j, :], start=(j == first_m[b] and q == 0),
-                                     stop=(j == last_m[b] and q == 3))
+        def pool_tile(t):
+            b = t // TILES_PER_IMAGE
+            for q in range(C_BLOCKS):
+                nc.tensor.matmul(out=pooled[:, b, q, :], lhsT=product_of[t][:, q * P:(q + 1) * P],
+                                 rhs=weights[:, t, :], start=(t == opens_group[b] and q == 0),
+                                 stop=(t == closes_group[b] and q == C_BLOCKS - 1))
 
         for i in range(n_steps):
-            if i < NT:
-                t0 = i * P
-                kps = psum_k.tile([P, C], F32, tag="kps")
-                vps = psum_v.tile([P, C], F32, tag="vps")
-                for h, acc in ((0, kps), (1, vps)):
-                    nc.tensor.matmul_mx(
-                        out=acc[:],
-                        lhsT=x_codes[:, t0:t0 + P].bitcast(FP8X4),
-                        lhsT_scale=x_scales[:, t0:t0 + P],
-                        rhs=w_codes[:, h * C:(h + 1) * C].bitcast(FP8X4),
-                        rhs_scale=w_scales[:, h * C:(h + 1) * C],
-                        start=True, stop=True)
-                k_sb = work.tile([P, C], F32, tag="k_sb")
-                nc.vector.tensor_tensor(out=k_sb[:], in0=kps[:], in1=bias_b[:, 0:C], op=ALU.add)
-                v_sb = work.tile([P, C], F32, tag="v_sb")
-                junk = work.tile([P, C], BF16, tag="junk")
-                nc.scalar.activation(out=junk[:], in_=k_sb[:], func=ACT.Square, accum_out=n2[:, i:i + 1])
-            for f, n in weights_at.get(i, []):
-                nc.vector.reciprocal(out=rn[:, f:f + n], in_=nrm[:, f:f + n])
-            if i < NT:
-                nc.vector.tensor_tensor(out=v_sb[:], in0=vps[:], in1=bias_b[:, C:2 * C], op=ALU.add)
-                p_sb = prod.tile([P, C], F32, tag="p_sb")
-                nc.gpsimd.tensor_tensor(out=p_sb[:], in0=k_sb[:], in1=v_sb[:], op=ALU.mult)
-                held[i] = p_sb
-            for f, n in sqrt_at.get(i, []):
-                nc.scalar.activation(out=nrm[:, f:f + n], in_=n2[:, f:f + n], func=ACT.Sqrt)
-            for j in scale_at.get(i, []):
-                scale(j)
+            if i < N_TILES:
+                pixels = slice(i * P, (i + 1) * P)
+                k_bank = psum_k.tile([P, C], F32, tag="k_bank")
+                v_bank = psum_v.tile([P, C], F32, tag="v_bank")
+                for h, bank in ((0, k_bank), (1, v_bank)):
+                    nc.tensor.matmul_mx(out=bank[:],
+                                        lhsT=x_codes[:, pixels].bitcast(FP8X4), lhsT_scale=x_scales[:, pixels],
+                                        rhs=w_codes[:, h * C:(h + 1) * C].bitcast(FP8X4),
+                                        rhs_scale=w_scales[:, h * C:(h + 1) * C], start=True, stop=True)
+                if i % 2 == 0:
+                    k_pair = work.tile([P, 2, C], F32, tag="k_pair")
+                    v_pair = work.tile([P, 2, C], F32, tag="v_pair")
+                nc.vector.tensor_tensor(out=k_pair[:, i % 2, :], in0=k_bank[:], in1=bias_rows[:, 0:C], op=ALU.add)
+                squares = work.tile([P, C], BF16, tag="squares")
+                nc.scalar.activation(out=squares[:], in_=k_pair[:, i % 2, :], func=ACT.Square,
+                                     accum_out=norm_sq[:, i:i + 1])
+            for f, size in weights_at.get(i, []):
+                nc.vector.reciprocal(out=inv_norm[:, f:f + size], in_=norm[:, f:f + size])
+            if i < N_TILES:
+                nc.vector.tensor_tensor(out=v_pair[:, i % 2, :], in0=v_bank[:], in1=bias_rows[:, C:2 * C],
+                                        op=ALU.add)
+                if i % 2 == 1:
+                    product = products.tile([P, 2, C], F32, tag="product")
+                    nc.gpsimd.tensor_tensor(out=product[:], in0=k_pair[:], in1=v_pair[:], op=ALU.mult)
+                    product_of[i - 1] = product[:, 0, :]
+                    product_of[i] = product[:, 1, :]
+            for f, size in sqrt_at.get(i, []):
+                nc.scalar.activation(out=norm[:, f:f + size], in_=norm_sq[:, f:f + size], func=ACT.Sqrt)
             if i in piece_at:
                 regroup_piece(piece_at[i][0], piece_at[i][1])
-            if i in quant_at:
-                quantise_chunk(quant_at[i])
+            if i in quantise_at:
+                quantise_chunk(quantise_at[i])
             if i == 1:
-                nc.vector.tensor_copy(out=mk_f[:], in_=mk_raw[:])
+                nc.vector.tensor_copy(out=mask_f32[:], in_=mask_rows[:])
             if i == 2:
-                mk_ps = psum_k.tile([P, C], F32, tag="kps", name="mk_ps")
-                nc.tensor.transpose(mk_ps[:, 0:P], mk_f[:], ident[:])
+                mask_bank = psum_k.tile([P, C], F32, tag="k_bank", name="mask_bank")
+                nc.tensor.transpose(mask_bank[:, 0:P], mask_f32[:], ident[:])
             if i == 3:
-                nc.vector.tensor_copy(out=mo[:, :, 1], in_=mk_ps[:, 0:NT])
-                nc.vector.tensor_scalar(out=mo[:, :, 0], in0=mk_ps[:, 0:NT], scalar1=-1.0, scalar2=1.0,
-                                        op0=ALU.mult, op1=ALU.add)
-            for f, n in weights_at.get(i, []):
-                nc.vector.tensor_tensor(out=w_t[:, f:f + n, 0:2], in0=mo[:, f:f + n, :],
-                                        in1=rn[:, f:f + n].unsqueeze(2).to_broadcast([P, n, 2]), op=ALU.mult)
-            for j in back_at.get(i, []):
-                back(j)
+                nc.vector.tensor_copy(out=mask_pair[:, :, 1], in_=mask_bank[:, 0:N_TILES])
+                nc.vector.tensor_scalar(out=mask_pair[:, :, 0], in0=mask_bank[:, 0:N_TILES], scalar1=-1.0,
+                                        scalar2=1.0, op0=ALU.mult, op1=ALU.add)
+            for f, size in weights_at.get(i, []):
+                nc.vector.tensor_tensor(out=weights[:, f:f + size, 0:2], in0=mask_pair[:, f:f + size, :],
+                                        in1=inv_norm[:, f:f + size].unsqueeze(2).to_broadcast([P, size, 2]),
+                                        op=ALU.mult)
+            for t in pool_at.get(i, []):
+                pool_tile(t)
 
         for b in range(B):
-            nc.vector.tensor_tensor(
-                out=res[:, 0:16].rearrange("p (j b q) -> p j b q", j=2, b=B)[:, :, b, :],
-                in0=red[:, b, :, 0:2].rearrange("p q j -> p j q"),
-                in1=acc_sum[:, :, b, :], op=ALU.add)
-        res_ps = psum_k.tile([P, C], F32, tag="kps", name="res_ps")
-        nc.tensor.transpose(res_ps[:, 0:P], res[:], ident[:])
-        res_t = const.tile([16, P], F32)
-        nc.scalar.copy(out=res_t[:], in_=res_ps[0:16, 0:P])
-        nc.sync.dma_start(out=out_0.rearrange("b o (q p) -> (b o q) p", p=P), in_=res_t[0:8, :])
-        nc.sync.dma_start(out=out_1.rearrange("b o (q p) -> (b o q) p", p=P), in_=res_t[8:16, :])
+            nc.vector.tensor_copy(out=result[:, 0:16].rearrange("p (j b q) -> p j b q", j=2, b=B)[:, :, b, :],
+                                  in_=pooled[:, b, :, 0:2].rearrange("p q j -> p j q"))
+        result_bank = psum_k.tile([P, C], F32, tag="k_bank", name="result_bank")
+        nc.tensor.transpose(result_bank[:, 0:P], result[:], ident[:])
+        result_rows = const.tile([16, P], F32)
+        nc.scalar.copy(out=result_rows[:], in_=result_bank[0:16, 0:P])
+        nc.sync.dma_start(out=out_0.rearrange("b o (q p) -> (b o q) p", p=P), in_=result_rows[0:8, :])
+        nc.sync.dma_start(out=out_1.rearrange("b o (q p) -> (b o q) p", p=P), in_=result_rows[8:16, :])

@@ -23,22 +23,31 @@ FLOPS = 2 * B * T * C * (2 * C)
 
 POOL_COLS = 64
 
-CHUNKS = [(0, 0, 256), (0, 256, 256), (0, 512, 512), (0, 1024, 1024), (0, 2048, 1024), (0, 3072, 1024),
-          (1, 0, 1024), (1, 1024, 1024), (1, 2048, 1024), (1, 3072, 1024)]
-MAX_CHUNK = 1024
 PIECE = 256
-CHUNK_LEAD = 10
+N_PIECES = B * T // PIECE
+PIECES_PER_IMAGE = T // PIECE
 
-GROUPS = [4] * 14 + [2, 2, 2, 1, 1]
-DISTANCES = {4: (1, 4, 6), 2: (1, 3, 5), 1: (1, 3, 5)}
+GROUP = 4
+SQRT_AFTER = 1
+WEIGHTS_AFTER = 4
+POOL_AFTER = GROUP - 1 + WEIGHTS_AFTER + 2
 PRODUCT_BUFS = 7
+
+
+def regroup_step(r):
+    return max(r - 2, 2 * r - 8)
+
+
+def group_due(step, distance):
+    last = step - distance
+    return last - (GROUP - 1) if 0 <= last < N_TILES and last % GROUP == GROUP - 1 else None
 
 
 def tile_hydraattention_pa_t_kernel(tc, x, mask, W_kv, b_kv, out_0, out_1):
     nc = tc.nc
     with ExitStack() as ctx:
         const = ctx.enter_context(tc.tile_pool(name="const", bufs=1))
-        stage = ctx.enter_context(tc.tile_pool(name="stage", bufs=2))
+        stage = ctx.enter_context(tc.tile_pool(name="stage", bufs=4))
         work = ctx.enter_context(tc.tile_pool(name="work", bufs=3))
         products = ctx.enter_context(tc.tile_pool(name="products", bufs=PRODUCT_BUFS))
         psum_k = ctx.enter_context(tc.psum_pool(name="psum_k", bufs=3))
@@ -47,23 +56,22 @@ def tile_hydraattention_pa_t_kernel(tc, x, mask, W_kv, b_kv, out_0, out_1):
         ctx.enter_context(tc.manual_schedule())
 
         w_raw = [const.tile([P, PACK, C], BF16, name="w_raw%d" % h) for h in range(2)]
-        x_raw = [const.tile([P, PACK, width], BF16, name="x_raw%d" % ci)
-                 for ci, (b, p0, width) in enumerate(CHUNKS)]
+        x_raw = [const.tile([P, PACK, PIECE], BF16, name="x_raw%d" % r) for r in range(N_PIECES)]
 
         def load_w(h):
             nc.sync.dma_start(out=w_raw[h][:],
                               in_=W_kv.rearrange("(p j) n -> p j n", j=PACK)[:, :, h * C:(h + 1) * C])
 
-        def load_x(ci):
-            b, p0, width = CHUNKS[ci]
-            nc.sync.dma_start(out=x_raw[ci][:],
-                              in_=x[b].rearrange("(p j) h w -> p j (h w)", j=PACK)[:, :, p0:p0 + width])
+        def load_x(r):
+            b, p0 = r // PIECES_PER_IMAGE, (r % PIECES_PER_IMAGE) * PIECE
+            nc.sync.dma_start(out=x_raw[r][:],
+                              in_=x[b].rearrange("(p j) h w -> p j (h w)", j=PACK)[:, :, p0:p0 + PIECE])
 
         load_w(0)
         load_x(0)
         load_w(1)
-        for ci in range(1, len(CHUNKS)):
-            load_x(ci)
+        for r in range(1, N_PIECES):
+            load_x(r)
         bias_rows = const.tile([P, 2 * C], BF16)
         nc.scalar.dma_start(out=bias_rows[:], in_=b_kv.partition_broadcast(P))
         mask_rows = const.tile([P, P], BF16)
@@ -91,18 +99,14 @@ def tile_hydraattention_pa_t_kernel(tc, x, mask, W_kv, b_kv, out_0, out_1):
         def regroup(copy, dst, src):
             copy(out=dst.rearrange("p (c i) j -> p c j i", i=4), in_=src.rearrange("p j (c i) -> p c j i", i=4))
 
-        def regroup_piece(ci, first_pixel):
-            if first_pixel == 0:
-                x_grouped[ci] = stage.tile([P, MAX_CHUNK, PACK], BF16, align_bytes=64, tag="x_grouped",
-                                           name="x_grouped")
-            cols = slice(first_pixel, first_pixel + PIECE)
-            regroup(nc.scalar.copy, x_grouped[ci][:, cols, :], x_raw[ci][:, :, cols])
+        def regroup_piece(r):
+            x_grouped[r] = stage.tile([P, PIECE, PACK], BF16, align_bytes=64, tag="x_grouped", name="x_grouped")
+            regroup(nc.scalar.copy, x_grouped[r][:], x_raw[r][:])
 
-        def quantise_chunk(ci):
-            b, p0, width = CHUNKS[ci]
-            cols = slice(b * T + p0, b * T + p0 + width)
+        def quantise_piece(r):
+            cols = slice(r * PIECE, (r + 1) * PIECE)
             nc.vector.quantize_mx(out=x_codes[:, cols].bitcast(FP8X4), scales=x_scales[:, cols],
-                                  in_=x_grouped[ci][:, 0:width, :].rearrange("p w j -> p (w j)"))
+                                  in_=x_grouped[r][:].rearrange("p w j -> p (w j)"))
 
         def quantise_w(h):
             cols = slice(h * C, (h + 1) * C)
@@ -110,40 +114,13 @@ def tile_hydraattention_pa_t_kernel(tc, x, mask, W_kv, b_kv, out_0, out_1):
                                   in_=w_grouped[:, cols, :].rearrange("p w j -> p (w j)"))
 
         regroup(nc.vector.tensor_copy, w_grouped[:, 0:C, :], w_raw[0][:])
-        regroup_piece(0, 0)
+        regroup_piece(0)
         regroup(nc.scalar.copy, w_grouped[:, C:C + C // 2, :], w_raw[1][:, :, 0:C // 2])
         quantise_w(0)
-        quantise_chunk(0)
+        quantise_piece(0)
         regroup(nc.vector.tensor_copy, w_grouped[:, C + C // 2:2 * C, :], w_raw[1][:, :, C // 2:C])
-        regroup_piece(1, 0)
+        regroup_piece(1)
         quantise_w(1)
-
-        piece_at = {}
-        quantise_at = {0: 1}
-        free_step = 0
-        for ci in range(2, len(CHUNKS)):
-            b, p0, width = CHUNKS[ci]
-            begin = max(free_step, (b * T + p0) // P - CHUNK_LEAD)
-            for n in range(width // PIECE):
-                piece_at[begin + n] = (ci, n * PIECE)
-            free_step = begin + width // PIECE
-            quantise_at[free_step + (0 if ci <= 3 else 1)] = ci
-        sqrt_at = {}
-        weights_at = {}
-        pool_at = {}
-        first = 0
-        for size in GROUPS:
-            last = first + size - 1
-            d_sqrt, d_weights, d_pool = DISTANCES[size]
-            sqrt_at[last + d_sqrt] = sqrt_at.get(last + d_sqrt, []) + [(first, size)]
-            weights_at[last + d_weights] = weights_at.get(last + d_weights, []) + [(first, size)]
-            for n in range(size):
-                pool_at[last + d_pool + n] = pool_at.get(last + d_pool + n, []) + [first + n]
-            first += size
-        n_steps = max(pool_at) + 1
-        pool_order = [t for i in range(n_steps) for t in pool_at.get(i, [])]
-        opens_group = [[t for t in pool_order if t // TILES_PER_IMAGE == b][0] for b in range(B)]
-        closes_group = [[t for t in pool_order if t // TILES_PER_IMAGE == b][-1] for b in range(B)]
 
         mask_f32 = const.tile([P, P], F32)
         mask_pair = const.tile([P, N_TILES, 2], F32)
@@ -157,10 +134,10 @@ def tile_hydraattention_pa_t_kernel(tc, x, mask, W_kv, b_kv, out_0, out_1):
             b = t // TILES_PER_IMAGE
             for q in range(C_BLOCKS):
                 nc.tensor.matmul(out=pooled[:, b, q, :], lhsT=product_of[t][:, q * P:(q + 1) * P],
-                                 rhs=weights[:, t, :], start=(t == opens_group[b] and q == 0),
-                                 stop=(t == closes_group[b] and q == C_BLOCKS - 1))
+                                 rhs=weights[:, t, :], start=(t % TILES_PER_IMAGE == 0 and q == 0),
+                                 stop=(t % TILES_PER_IMAGE == TILES_PER_IMAGE - 1 and q == C_BLOCKS - 1))
 
-        for i in range(n_steps):
+        for i in range(N_TILES + POOL_AFTER):
             if i < N_TILES:
                 pixels = slice(i * P, (i + 1) * P)
                 k_bank = psum_k.tile([P, C], F32, tag="k_bank")
@@ -177,8 +154,9 @@ def tile_hydraattention_pa_t_kernel(tc, x, mask, W_kv, b_kv, out_0, out_1):
                 squares = work.tile([P, C], BF16, tag="squares")
                 nc.scalar.activation(out=squares[:], in_=k_pair[:, i % 2, :], func=ACT.Square,
                                      accum_out=norm_sq[:, i:i + 1])
-            for f, size in weights_at.get(i, []):
-                nc.vector.reciprocal(out=inv_norm[:, f:f + size], in_=norm[:, f:f + size])
+            f = group_due(i, WEIGHTS_AFTER)
+            if f is not None:
+                nc.vector.reciprocal(out=inv_norm[:, f:f + GROUP], in_=norm[:, f:f + GROUP])
             if i < N_TILES:
                 nc.vector.tensor_tensor(out=v_pair[:, i % 2, :], in0=v_bank[:], in1=bias_rows[:, C:2 * C],
                                         op=ALU.add)
@@ -187,12 +165,14 @@ def tile_hydraattention_pa_t_kernel(tc, x, mask, W_kv, b_kv, out_0, out_1):
                     nc.gpsimd.tensor_tensor(out=product[:], in0=k_pair[:], in1=v_pair[:], op=ALU.mult)
                     product_of[i - 1] = product[:, 0, :]
                     product_of[i] = product[:, 1, :]
-            for f, size in sqrt_at.get(i, []):
-                nc.scalar.activation(out=norm[:, f:f + size], in_=norm_sq[:, f:f + size], func=ACT.Sqrt)
-            if i in piece_at:
-                regroup_piece(piece_at[i][0], piece_at[i][1])
-            if i in quantise_at:
-                quantise_chunk(quantise_at[i])
+            s = group_due(i, SQRT_AFTER)
+            if s is not None:
+                nc.scalar.activation(out=norm[:, s:s + GROUP], in_=norm_sq[:, s:s + GROUP], func=ACT.Sqrt)
+            for r in range(N_PIECES):
+                if regroup_step(r) == i:
+                    regroup_piece(r)
+                if regroup_step(r) + 1 == i:
+                    quantise_piece(r)
             if i == 1:
                 nc.vector.tensor_copy(out=mask_f32[:], in_=mask_rows[:])
             if i == 2:
@@ -202,12 +182,12 @@ def tile_hydraattention_pa_t_kernel(tc, x, mask, W_kv, b_kv, out_0, out_1):
                 nc.vector.tensor_copy(out=mask_pair[:, :, 1], in_=mask_bank[:, 0:N_TILES])
                 nc.vector.tensor_scalar(out=mask_pair[:, :, 0], in0=mask_bank[:, 0:N_TILES], scalar1=-1.0,
                                         scalar2=1.0, op0=ALU.mult, op1=ALU.add)
-            for f, size in weights_at.get(i, []):
-                nc.vector.tensor_tensor(out=weights[:, f:f + size, 0:2], in0=mask_pair[:, f:f + size, :],
-                                        in1=inv_norm[:, f:f + size].unsqueeze(2).to_broadcast([P, size, 2]),
+            if f is not None:
+                nc.vector.tensor_tensor(out=weights[:, f:f + GROUP, 0:2], in0=mask_pair[:, f:f + GROUP, :],
+                                        in1=inv_norm[:, f:f + GROUP].unsqueeze(2).to_broadcast([P, GROUP, 2]),
                                         op=ALU.mult)
-            for t in pool_at.get(i, []):
-                pool_tile(t)
+            if i >= POOL_AFTER:
+                pool_tile(i - POOL_AFTER)
 
         for b in range(B):
             nc.vector.tensor_copy(out=result[:, 0:16].rearrange("p (j b q) -> p j b q", j=2, b=B)[:, :, b, :],

@@ -23,9 +23,11 @@ FLOPS = 2 * B * T * C * (2 * C)
 
 POOL_COLS = 64
 
+CHUNKS = [(0, 0, 256), (0, 256, 256), (0, 512, 512), (0, 1024, 1024), (0, 2048, 1024), (0, 3072, 1024),
+          (1, 0, 1024), (1, 1024, 1024), (1, 2048, 1024), (1, 3072, 1024)]
+MAX_CHUNK = 1024
 PIECE = 256
-N_PIECES = B * T // PIECE
-PIECES_PER_IMAGE = T // PIECE
+CHUNK_LEAD = 10
 
 GROUP = 4
 SQRT_AFTER = 1
@@ -34,8 +36,10 @@ POOL_AFTER = GROUP - 1 + WEIGHTS_AFTER + 2
 PRODUCT_BUFS = 7
 
 
-def regroup_step(r):
-    return max(r - 2, 2 * r - 8)
+def regroup_begin(ci):
+    b, p0, width = CHUNKS[ci]
+    first_pixel = b * T + p0
+    return max(first_pixel // PIECE - 2, first_pixel // P - CHUNK_LEAD)
 
 
 def group_due(step, distance):
@@ -47,7 +51,7 @@ def tile_hydraattention_pa_t_kernel(tc, x, mask, W_kv, b_kv, out_0, out_1):
     nc = tc.nc
     with ExitStack() as ctx:
         const = ctx.enter_context(tc.tile_pool(name="const", bufs=1))
-        stage = ctx.enter_context(tc.tile_pool(name="stage", bufs=4))
+        stage = ctx.enter_context(tc.tile_pool(name="stage", bufs=2))
         work = ctx.enter_context(tc.tile_pool(name="work", bufs=3))
         products = ctx.enter_context(tc.tile_pool(name="products", bufs=PRODUCT_BUFS))
         psum_k = ctx.enter_context(tc.psum_pool(name="psum_k", bufs=3))
@@ -56,22 +60,23 @@ def tile_hydraattention_pa_t_kernel(tc, x, mask, W_kv, b_kv, out_0, out_1):
         ctx.enter_context(tc.manual_schedule())
 
         w_raw = [const.tile([P, PACK, C], BF16, name="w_raw%d" % h) for h in range(2)]
-        x_raw = [const.tile([P, PACK, PIECE], BF16, name="x_raw%d" % r) for r in range(N_PIECES)]
+        x_raw = [const.tile([P, PACK, width], BF16, name="x_raw%d" % ci)
+                 for ci, (b, p0, width) in enumerate(CHUNKS)]
 
         def load_w(h):
             nc.sync.dma_start(out=w_raw[h][:],
                               in_=W_kv.rearrange("(p j) n -> p j n", j=PACK)[:, :, h * C:(h + 1) * C])
 
-        def load_x(r):
-            b, p0 = r // PIECES_PER_IMAGE, (r % PIECES_PER_IMAGE) * PIECE
-            nc.sync.dma_start(out=x_raw[r][:],
-                              in_=x[b].rearrange("(p j) h w -> p j (h w)", j=PACK)[:, :, p0:p0 + PIECE])
+        def load_x(ci):
+            b, p0, width = CHUNKS[ci]
+            nc.sync.dma_start(out=x_raw[ci][:],
+                              in_=x[b].rearrange("(p j) h w -> p j (h w)", j=PACK)[:, :, p0:p0 + width])
 
         load_w(0)
         load_x(0)
         load_w(1)
-        for r in range(1, N_PIECES):
-            load_x(r)
+        for ci in range(1, len(CHUNKS)):
+            load_x(ci)
         bias_rows = const.tile([P, 2 * C], BF16)
         nc.scalar.dma_start(out=bias_rows[:], in_=b_kv.partition_broadcast(P))
         mask_rows = const.tile([P, P], BF16)
@@ -99,14 +104,18 @@ def tile_hydraattention_pa_t_kernel(tc, x, mask, W_kv, b_kv, out_0, out_1):
         def regroup(copy, dst, src):
             copy(out=dst.rearrange("p (c i) j -> p c j i", i=4), in_=src.rearrange("p j (c i) -> p c j i", i=4))
 
-        def regroup_piece(r):
-            x_grouped[r] = stage.tile([P, PIECE, PACK], BF16, align_bytes=64, tag="x_grouped", name="x_grouped")
-            regroup(nc.scalar.copy, x_grouped[r][:], x_raw[r][:])
+        def regroup_piece(ci, n):
+            if n == 0:
+                x_grouped[ci] = stage.tile([P, MAX_CHUNK, PACK], BF16, align_bytes=64, tag="x_grouped",
+                                           name="x_grouped")
+            cols = slice(n * PIECE, (n + 1) * PIECE)
+            regroup(nc.scalar.copy, x_grouped[ci][:, cols, :], x_raw[ci][:, :, cols])
 
-        def quantise_piece(r):
-            cols = slice(r * PIECE, (r + 1) * PIECE)
+        def quantise_chunk(ci):
+            b, p0, width = CHUNKS[ci]
+            cols = slice(b * T + p0, b * T + p0 + width)
             nc.vector.quantize_mx(out=x_codes[:, cols].bitcast(FP8X4), scales=x_scales[:, cols],
-                                  in_=x_grouped[r][:].rearrange("p w j -> p (w j)"))
+                                  in_=x_grouped[ci][:, 0:width, :].rearrange("p w j -> p (w j)"))
 
         def quantise_w(h):
             cols = slice(h * C, (h + 1) * C)
@@ -114,12 +123,12 @@ def tile_hydraattention_pa_t_kernel(tc, x, mask, W_kv, b_kv, out_0, out_1):
                                   in_=w_grouped[:, cols, :].rearrange("p w j -> p (w j)"))
 
         regroup(nc.vector.tensor_copy, w_grouped[:, 0:C, :], w_raw[0][:])
-        regroup_piece(0)
+        regroup_piece(0, 0)
         regroup(nc.scalar.copy, w_grouped[:, C:C + C // 2, :], w_raw[1][:, :, 0:C // 2])
         quantise_w(0)
-        quantise_piece(0)
+        quantise_chunk(0)
         regroup(nc.vector.tensor_copy, w_grouped[:, C + C // 2:2 * C, :], w_raw[1][:, :, C // 2:C])
-        regroup_piece(1)
+        regroup_piece(1, 0)
         quantise_w(1)
 
         mask_f32 = const.tile([P, P], F32)
@@ -168,11 +177,13 @@ def tile_hydraattention_pa_t_kernel(tc, x, mask, W_kv, b_kv, out_0, out_1):
             s = group_due(i, SQRT_AFTER)
             if s is not None:
                 nc.scalar.activation(out=norm[:, s:s + GROUP], in_=norm_sq[:, s:s + GROUP], func=ACT.Sqrt)
-            for r in range(N_PIECES):
-                if regroup_step(r) == i:
-                    regroup_piece(r)
-                if regroup_step(r) + 1 == i:
-                    quantise_piece(r)
+            for ci in range(len(CHUNKS)):
+                n = i - regroup_begin(ci)
+                n_pieces = CHUNKS[ci][2] // PIECE
+                if 0 <= n < n_pieces:
+                    regroup_piece(ci, n)
+                if n == n_pieces:
+                    quantise_chunk(ci)
             if i == 1:
                 nc.vector.tensor_copy(out=mask_f32[:], in_=mask_rows[:])
             if i == 2:

@@ -23,23 +23,30 @@ FLOPS = 2 * B * T * C * (2 * C)
 
 POOL_COLS = 64
 
-CHUNKS = [(0, 0, 256), (0, 256, 256), (0, 512, 512), (0, 1024, 1024), (0, 2048, 1024), (0, 3072, 1024),
+CHUNKS = [(0, 0, 256), (0, 256, 256), (0, 512, 512), (0, 1024, 512), (0, 1536, 512), (0, 2048, 1024), (0, 3072, 1024),
           (1, 0, 1024), (1, 1024, 1024), (1, 2048, 1024), (1, 3072, 1024)]
 MAX_CHUNK = 1024
 PIECE = 256
 CHUNK_LEAD = 10
+QUANTISE_WAIT = 2
 
-GROUP = 4
-SQRT_AFTER = 1
-WEIGHTS_AFTER = 4
-POOL_AFTER = GROUP - 1 + WEIGHTS_AFTER + 2
-PRODUCT_BUFS = 7
+GROUP = 2
+SQRT_AFTER = 0
+WEIGHTS_AFTER = 2
+POOL_AFTER = GROUP - 1 + WEIGHTS_AFTER + 3
+PRODUCT_BUFS = 5
 
 
 def regroup_begin(ci):
     b, p0, width = CHUNKS[ci]
     first_pixel = b * T + p0
     return max(first_pixel // PIECE - 2, first_pixel // P - CHUNK_LEAD)
+
+
+def quantise_step(ci):
+    b, p0, width = CHUNKS[ci]
+    in_time = regroup_begin(ci) == (b * T + p0) // P - CHUNK_LEAD
+    return regroup_begin(ci) + width // PIECE + (QUANTISE_WAIT if in_time else 0)
 
 
 def group_due(step, distance):
@@ -163,6 +170,9 @@ def tile_hydraattention_pa_t_kernel(tc, x, mask, W_kv, b_kv, out_0, out_1):
                 squares = work.tile([P, C], BF16, tag="squares")
                 nc.scalar.activation(out=squares[:], in_=k_pair[:, i % 2, :], func=ACT.Square,
                                      accum_out=norm_sq[:, i:i + 1])
+            s = group_due(i, SQRT_AFTER)
+            if s is not None:
+                nc.scalar.activation(out=norm[:, s:s + GROUP], in_=norm_sq[:, s:s + GROUP], func=ACT.Sqrt)
             f = group_due(i, WEIGHTS_AFTER)
             if f is not None:
                 nc.vector.reciprocal(out=inv_norm[:, f:f + GROUP], in_=norm[:, f:f + GROUP])
@@ -174,15 +184,12 @@ def tile_hydraattention_pa_t_kernel(tc, x, mask, W_kv, b_kv, out_0, out_1):
                     nc.gpsimd.tensor_tensor(out=product[:], in0=k_pair[:], in1=v_pair[:], op=ALU.mult)
                     product_of[i - 1] = product[:, 0, :]
                     product_of[i] = product[:, 1, :]
-            s = group_due(i, SQRT_AFTER)
-            if s is not None:
-                nc.scalar.activation(out=norm[:, s:s + GROUP], in_=norm_sq[:, s:s + GROUP], func=ACT.Sqrt)
             for ci in range(len(CHUNKS)):
                 n = i - regroup_begin(ci)
                 n_pieces = CHUNKS[ci][2] // PIECE
                 if 0 <= n < n_pieces:
                     regroup_piece(ci, n)
-                if n == n_pieces:
+                if ci > 0 and i == quantise_step(ci):
                     quantise_chunk(ci)
             if i == 1:
                 nc.vector.tensor_copy(out=mask_f32[:], in_=mask_rows[:])

@@ -46,7 +46,8 @@ def regroup_begin(ci):
 def quantise_step(ci):
     b, p0, width = CHUNKS[ci]
     in_time = regroup_begin(ci) == (b * T + p0) // P - CHUNK_LEAD
-    return regroup_begin(ci) + width // PIECE + (QUANTISE_WAIT if in_time else 0)
+    step = regroup_begin(ci) + width // PIECE + (QUANTISE_WAIT if in_time else 0)
+    return step + 1 - step % 2
 
 
 def group_due(step, distance):
@@ -176,6 +177,9 @@ def tile_hydraattention_pa_t_kernel(tc, x, mask, W_kv, b_kv, out_0, out_1):
             f = group_due(i, WEIGHTS_AFTER)
             if f is not None:
                 nc.vector.reciprocal(out=inv_norm[:, f:f + GROUP], in_=norm[:, f:f + GROUP])
+            for ci in range(1, len(CHUNKS)):
+                if i == quantise_step(ci):
+                    quantise_chunk(ci)
             if i < N_TILES:
                 nc.vector.tensor_tensor(out=v_pair[:, i % 2, :], in0=v_bank[:], in1=bias_rows[:, C:2 * C],
                                         op=ALU.add)
@@ -189,8 +193,6 @@ def tile_hydraattention_pa_t_kernel(tc, x, mask, W_kv, b_kv, out_0, out_1):
                 n_pieces = CHUNKS[ci][2] // PIECE
                 if 0 <= n < n_pieces:
                     regroup_piece(ci, n)
-                if ci > 0 and i == quantise_step(ci):
-                    quantise_chunk(ci)
             if i == 1:
                 nc.vector.tensor_copy(out=mask_f32[:], in_=mask_rows[:])
             if i == 2:

@@ -147,14 +147,14 @@ def tile_hydraattention_pa_t_kernel(tc, x, mask, W_kv, b_kv, out_0, out_1):
         pooled = psum_pool.tile([P, B, C_BLOCKS, POOL_COLS], F32)
         product_of = {}
 
-        def pool_tile(t):
+        def pool_tile(t, blocks):
             b = t // TILES_PER_IMAGE
-            for q in range(C_BLOCKS):
+            for q in blocks:
                 nc.tensor.matmul(out=pooled[:, b, q, :], lhsT=product_of[t][:, q * P:(q + 1) * P],
                                  rhs=weights[:, t, :], start=(t % TILES_PER_IMAGE == 0 and q == 0),
                                  stop=(t % TILES_PER_IMAGE == TILES_PER_IMAGE - 1 and q == C_BLOCKS - 1))
 
-        for i in range(N_TILES + POOL_AFTER):
+        for i in range(N_TILES + POOL_AFTER + 1):
             if i < N_TILES:
                 pixels = slice(i * P, (i + 1) * P)
                 k_bank = psum_k.tile([P, C], F32, tag="k_bank")
@@ -164,6 +164,8 @@ def tile_hydraattention_pa_t_kernel(tc, x, mask, W_kv, b_kv, out_0, out_1):
                                         lhsT=x_codes[:, pixels].bitcast(FP8X4), lhsT_scale=x_scales[:, pixels],
                                         rhs=w_codes[:, h * C:(h + 1) * C].bitcast(FP8X4),
                                         rhs_scale=w_scales[:, h * C:(h + 1) * C], start=True, stop=True)
+                    if i > POOL_AFTER:
+                        pool_tile(i - POOL_AFTER - 1, range(2 * h, 2 * h + 2))
                 if i % 2 == 0:
                     k_pair = work.tile([P, 2, C], F32, tag="k_pair")
                     v_pair = work.tile([P, 2, C], F32, tag="v_pair")
@@ -206,8 +208,8 @@ def tile_hydraattention_pa_t_kernel(tc, x, mask, W_kv, b_kv, out_0, out_1):
                 nc.vector.tensor_tensor(out=weights[:, f:f + GROUP, 0:2], in0=mask_pair[:, f:f + GROUP, :],
                                         in1=inv_norm[:, f:f + GROUP].unsqueeze(2).to_broadcast([P, GROUP, 2]),
                                         op=ALU.mult)
-            if i >= POOL_AFTER:
-                pool_tile(i - POOL_AFTER)
+            if i >= N_TILES:
+                pool_tile(i - POOL_AFTER - 1, range(C_BLOCKS))
 
         for b in range(B):
             nc.vector.tensor_copy(out=result[:, 0:16].rearrange("p (j b q) -> p j b q", j=2, b=B)[:, :, b, :],

@@ -160,12 +160,14 @@ def tile_hydraattention_pa_t_kernel(tc, x, mask, W_kv, b_kv, out_0, out_1):
                 k_bank = psum_k.tile([P, C], F32, tag="k_bank")
                 v_bank = psum_v.tile([P, C], F32, tag="v_bank")
                 for h, bank in ((0, k_bank), (1, v_bank)):
-                    nc.tensor.matmul_mx(out=bank[:],
-                                        lhsT=x_codes[:, pixels].bitcast(FP8X4), lhsT_scale=x_scales[:, pixels],
-                                        rhs=w_codes[:, h * C:(h + 1) * C].bitcast(FP8X4),
-                                        rhs_scale=w_scales[:, h * C:(h + 1) * C], start=True, stop=True)
-                    if i > POOL_AFTER:
-                        pool_tile(i - POOL_AFTER - 1, range(2 * h, 2 * h + 2))
+                    for half in range(2):
+                        cols = slice(h * C + half * (C // 2), h * C + (half + 1) * (C // 2))
+                        nc.tensor.matmul_mx(out=bank[:, half * (C // 2):(half + 1) * (C // 2)],
+                                            lhsT=x_codes[:, pixels].bitcast(FP8X4), lhsT_scale=x_scales[:, pixels],
+                                            rhs=w_codes[:, cols].bitcast(FP8X4), rhs_scale=w_scales[:, cols],
+                                            start=True, stop=True)
+                        if i > POOL_AFTER:
+                            pool_tile(i - POOL_AFTER - 1, range(2 * h + half, 2 * h + half + 1))
                 if i % 2 == 0:
                     k_pair = work.tile([P, 2, C], F32, tag="k_pair")
                     v_pair = work.tile([P, 2, C], F32, tag="v_pair")

@@ -31,9 +31,8 @@ CHUNK_LEAD = 10
 QUANTISE_WAIT = 2
 
 GROUP = 2
-SQRT_AFTER = 0
-WEIGHTS_AFTER = 2
-POOL_AFTER = GROUP - 1 + WEIGHTS_AFTER + 3
+MASK_STEP = 3
+POOL_AFTER = 6
 PRODUCT_BUFS = 5
 
 
@@ -94,7 +93,7 @@ def tile_hydraattention_pa_t_kernel(tc, x, mask, W_kv, b_kv, out_0, out_1):
 
         warm = const.tile([P, 1], F32)
         nc.vector.memset(warm[:], 1.0)
-        nc.scalar.activation(out=warm[:], in_=warm[:], func=ACT.Sqrt)
+        nc.scalar.activation(out=warm[:], in_=warm[:], func=ACT.Abs_reciprocal_sqrt)
         ident = const.tile([P, P], F32)
         make_identity(nc, ident[:])
         result = const.tile([P, P], F32)
@@ -142,7 +141,6 @@ def tile_hydraattention_pa_t_kernel(tc, x, mask, W_kv, b_kv, out_0, out_1):
         mask_f32 = const.tile([P, P], F32)
         mask_pair = const.tile([P, N_TILES, 2], F32)
         norm_sq = const.tile([P, N_TILES], F32)
-        norm = const.tile([P, N_TILES], F32)
         inv_norm = const.tile([P, N_TILES], F32)
         pooled = psum_pool.tile([P, B, C_BLOCKS, POOL_COLS], F32)
         product_of = {}
@@ -175,18 +173,20 @@ def tile_hydraattention_pa_t_kernel(tc, x, mask, W_kv, b_kv, out_0, out_1):
                 squares = work.tile([P, C], BF16, tag="squares")
                 nc.scalar.activation(out=squares[:], in_=k_pair[:, i % 2, :], func=ACT.Square,
                                      accum_out=norm_sq[:, i:i + 1])
-            s = group_due(i, SQRT_AFTER)
-            if s is not None:
-                nc.scalar.activation(out=norm[:, s:s + GROUP], in_=norm_sq[:, s:s + GROUP], func=ACT.Sqrt)
-            f = group_due(i, WEIGHTS_AFTER)
-            if f is not None:
-                nc.vector.reciprocal(out=inv_norm[:, f:f + GROUP], in_=norm[:, f:f + GROUP])
+            for s in range(0, N_TILES, GROUP):
+                if i == max(s + GROUP - 1, MASK_STEP + 1):
+                    nc.scalar.activation(out=inv_norm[:, s:s + GROUP], in_=norm_sq[:, s:s + GROUP],
+                                         func=ACT.Abs_reciprocal_sqrt)
+                    for t in range(s, s + GROUP):
+                        nc.scalar.activation(out=weights[:, t, 0:2], in_=mask_pair[:, t, :], func=ACT.Copy,
+                                             scale=inv_norm[:, t:t + 1])
+            if i < N_TILES:
+                nc.vector.tensor_tensor(out=v_pair[:, i % 2, :], in0=v_bank[:], in1=bias_rows[:, C:2 * C],
+                                        op=ALU.add)
             for ci in range(1, len(CHUNKS)):
                 if i == quantise_step(ci):
                     quantise_chunk(ci)
             if i < N_TILES:
-                nc.vector.tensor_tensor(out=v_pair[:, i % 2, :], in0=v_bank[:], in1=bias_rows[:, C:2 * C],
-                                        op=ALU.add)
                 if i % 2 == 1:
                     product = products.tile([P, 2, C], F32, tag="product")
                     nc.gpsimd.tensor_tensor(out=product[:], in0=k_pair[:], in1=v_pair[:], op=ALU.mult)
@@ -202,14 +202,10 @@ def tile_hydraattention_pa_t_kernel(tc, x, mask, W_kv, b_kv, out_0, out_1):
             if i == 2:
                 mask_bank = psum_k.tile([P, C], F32, tag="k_bank", name="mask_bank")
                 nc.tensor.transpose(mask_bank[:, 0:P], mask_f32[:], ident[:])
-            if i == 3:
+            if i == MASK_STEP:
                 nc.vector.tensor_copy(out=mask_pair[:, :, 1], in_=mask_bank[:, 0:N_TILES])
                 nc.vector.tensor_scalar(out=mask_pair[:, :, 0], in0=mask_bank[:, 0:N_TILES], scalar1=-1.0,
                                         scalar2=1.0, op0=ALU.mult, op1=ALU.add)
-            if f is not None:
-                nc.vector.tensor_tensor(out=weights[:, f:f + GROUP, 0:2], in0=mask_pair[:, f:f + GROUP, :],
-                                        in1=inv_norm[:, f:f + GROUP].unsqueeze(2).to_broadcast([P, GROUP, 2]),
-                                        op=ALU.mult)
             if i >= N_TILES:
                 pool_tile(i - POOL_AFTER - 1, range(C_BLOCKS))
 

@@ -32,6 +32,12 @@ QUANTISE_WAIT = 2
 
 GROUP = 2
 MASK_STEP = 3
+SPLIT_FROM = N_TILES - 4
+SPLIT_EVERY = 4
+FIRST_SPLIT = 5
+SPLIT_TILES = list(range(FIRST_SPLIT, SPLIT_FROM, SPLIT_EVERY)) + list(range(SPLIT_FROM, N_TILES))
+HIGH_AFTER = 2
+LOW_AFTER = 4
 POOL_AFTER = 6
 PRODUCT_BUFS = 5
 
@@ -60,6 +66,7 @@ def tile_hydraattention_pa_t_kernel(tc, x, mask, W_kv, b_kv, out_0, out_1):
         const = ctx.enter_context(tc.tile_pool(name="const", bufs=1))
         stage = ctx.enter_context(tc.tile_pool(name="stage", bufs=2))
         work = ctx.enter_context(tc.tile_pool(name="work", bufs=3))
+        halves = ctx.enter_context(tc.tile_pool(name="halves", bufs=4))
         products = ctx.enter_context(tc.tile_pool(name="products", bufs=PRODUCT_BUFS))
         psum_k = ctx.enter_context(tc.psum_pool(name="psum_k", bufs=3))
         psum_v = ctx.enter_context(tc.psum_pool(name="psum_v", bufs=4))
@@ -101,6 +108,12 @@ def tile_hydraattention_pa_t_kernel(tc, x, mask, W_kv, b_kv, out_0, out_1):
         weights = const.tile([P, N_TILES, POOL_COLS], F32)
         nc.gpsimd.memset(weights[:], 0.0)
 
+        one_and_mask = const.tile([P, N_TILES, 2], F32)
+        nc.vector.memset(one_and_mask[:], 1.0)
+        split_weights = const.tile([P, len(SPLIT_TILES), POOL_COLS], BF16)
+        nc.vector.memset(split_weights[:], 0.0)
+        nc.vector.memset(split_weights[:, :, 0:1], 1.0)
+
         w_grouped = const.tile([P, 2 * C, PACK], BF16, align_bytes=64)
         w_codes = const.tile([P, 2 * C], U32, align_bytes=64)
         w_scales = const.tile([P, 2 * C], U8, align_bytes=64)
@@ -139,18 +152,34 @@ def tile_hydraattention_pa_t_kernel(tc, x, mask, W_kv, b_kv, out_0, out_1):
         quantise_w(1)
 
         mask_f32 = const.tile([P, P], F32)
-        mask_pair = const.tile([P, N_TILES, 2], F32)
         norm_sq = const.tile([P, N_TILES], F32)
         inv_norm = const.tile([P, N_TILES], F32)
         pooled = psum_pool.tile([P, B, C_BLOCKS, POOL_COLS], F32)
         product_of = {}
+        split_of = {}
 
         def pool_tile(t, blocks):
             b = t // TILES_PER_IMAGE
+            parts = split_of[t] if t in SPLIT_TILES else [product_of[t]]
+            rhs = split_weights[:, SPLIT_TILES.index(t), :] if t in SPLIT_TILES else weights[:, t, :]
             for q in blocks:
-                nc.tensor.matmul(out=pooled[:, b, q, :], lhsT=product_of[t][:, q * P:(q + 1) * P],
-                                 rhs=weights[:, t, :], start=(t % TILES_PER_IMAGE == 0 and q == 0),
-                                 stop=(t % TILES_PER_IMAGE == TILES_PER_IMAGE - 1 and q == C_BLOCKS - 1))
+                for part in parts:
+                    nc.tensor.matmul(out=pooled[:, b, q, :], lhsT=part[:, q * P:(q + 1) * P], rhs=rhs,
+                                     start=(t % TILES_PER_IMAGE == 0 and q == 0),
+                                     stop=(t % TILES_PER_IMAGE == TILES_PER_IMAGE - 1 and q == C_BLOCKS - 1
+                                           and part is parts[-1]))
+
+        def high_part(t):
+            high = halves.tile([P, C], BF16, tag="high")
+            nc.scalar.activation(out=high[:], in_=product_of[t], func=ACT.Copy, scale=inv_norm[:, t:t + 1])
+            split_of[t] = [high]
+
+        def low_part(t):
+            high = split_of[t][0]
+            low = halves.tile([P, C], BF16, tag="low")
+            nc.vector.scalar_tensor_tensor(out=low[:], in0=product_of[t], scalar=inv_norm[:, t:t + 1], in1=high[:],
+                                           op0=ALU.mult, op1=ALU.subtract)
+            split_of[t].append(low)
 
         for i in range(N_TILES + POOL_AFTER + 1):
             if i < N_TILES:
@@ -177,8 +206,8 @@ def tile_hydraattention_pa_t_kernel(tc, x, mask, W_kv, b_kv, out_0, out_1):
                 if i == max(s + GROUP - 1, MASK_STEP + 1):
                     nc.scalar.activation(out=inv_norm[:, s:s + GROUP], in_=norm_sq[:, s:s + GROUP],
                                          func=ACT.Abs_reciprocal_sqrt)
-                    for t in range(s, s + GROUP):
-                        nc.scalar.activation(out=weights[:, t, 0:2], in_=mask_pair[:, t, :], func=ACT.Copy,
+                    for t in [t for t in range(s, s + GROUP) if t not in SPLIT_TILES]:
+                        nc.scalar.activation(out=weights[:, t, 0:2], in_=one_and_mask[:, t, :], func=ACT.Copy,
                                              scale=inv_norm[:, t:t + 1])
             if i < N_TILES:
                 nc.vector.tensor_tensor(out=v_pair[:, i % 2, :], in0=v_bank[:], in1=bias_rows[:, C:2 * C],
@@ -186,12 +215,21 @@ def tile_hydraattention_pa_t_kernel(tc, x, mask, W_kv, b_kv, out_0, out_1):
             for ci in range(1, len(CHUNKS)):
                 if i == quantise_step(ci):
                     quantise_chunk(ci)
+            if SPLIT_TILES[0] <= i - LOW_AFTER < SPLIT_FROM and i - LOW_AFTER in SPLIT_TILES:
+                low_part(i - LOW_AFTER)
             if i < N_TILES:
                 if i % 2 == 1:
                     product = products.tile([P, 2, C], F32, tag="product")
-                    nc.gpsimd.tensor_tensor(out=product[:], in0=k_pair[:], in1=v_pair[:], op=ALU.mult)
+                    if i < N_TILES - 1:
+                        nc.gpsimd.tensor_tensor(out=product[:], in0=k_pair[:], in1=v_pair[:], op=ALU.mult)
+                    else:
+                        for e in range(2):
+                            nc.vector.tensor_tensor(out=product[:, e, :], in0=k_pair[:, e, :], in1=v_pair[:, e, :],
+                                                    op=ALU.mult)
                     product_of[i - 1] = product[:, 0, :]
                     product_of[i] = product[:, 1, :]
+            if i - HIGH_AFTER < SPLIT_FROM and i - HIGH_AFTER in SPLIT_TILES:
+                high_part(i - HIGH_AFTER)
             for ci in range(len(CHUNKS)):
                 n = i - regroup_begin(ci)
                 n_pieces = CHUNKS[ci][2] // PIECE
@@ -203,15 +241,22 @@ def tile_hydraattention_pa_t_kernel(tc, x, mask, W_kv, b_kv, out_0, out_1):
                 mask_bank = psum_k.tile([P, C], F32, tag="k_bank", name="mask_bank")
                 nc.tensor.transpose(mask_bank[:, 0:P], mask_f32[:], ident[:])
             if i == MASK_STEP:
-                nc.vector.tensor_copy(out=mask_pair[:, :, 1], in_=mask_bank[:, 0:N_TILES])
-                nc.vector.tensor_scalar(out=mask_pair[:, :, 0], in0=mask_bank[:, 0:N_TILES], scalar1=-1.0,
-                                        scalar2=1.0, op0=ALU.mult, op1=ALU.add)
+                nc.vector.tensor_copy(out=one_and_mask[:, :, 1], in_=mask_bank[:, 0:N_TILES])
+                n_spread = len(range(FIRST_SPLIT, SPLIT_FROM, SPLIT_EVERY))
+                nc.vector.tensor_copy(out=split_weights[:, 0:n_spread, 1], in_=mask_bank[:, FIRST_SPLIT:SPLIT_FROM:SPLIT_EVERY])
+                nc.vector.tensor_copy(out=split_weights[:, n_spread:, 1], in_=mask_bank[:, SPLIT_FROM:N_TILES])
+            if i == N_TILES - 1:
+                for t in range(SPLIT_FROM, N_TILES):
+                    high_part(t)
+                    low_part(t)
             if i >= N_TILES:
                 pool_tile(i - POOL_AFTER - 1, range(C_BLOCKS))
 
         for b in range(B):
-            nc.vector.tensor_copy(out=result[:, 0:16].rearrange("p (j b q) -> p j b q", j=2, b=B)[:, :, b, :],
-                                  in_=pooled[:, b, :, 0:2].rearrange("p q j -> p j q"))
+            mask_sums = result[:, 8 + 4 * b:8 + 4 * (b + 1)]
+            nc.vector.tensor_copy(out=mask_sums, in_=pooled[:, b, :, 1])
+            nc.vector.tensor_tensor(out=result[:, 4 * b:4 * (b + 1)], in0=pooled[:, b, :, 0], in1=mask_sums,
+                                    op=ALU.subtract)
         result_bank = psum_k.tile([P, C], F32, tag="k_bank", name="result_bank")
         nc.tensor.transpose(result_bank[:, 0:P], result[:], ident[:])
         result_rows = const.tile([16, P], F32)

@@ -27,19 +27,23 @@ CHUNKS = [(0, 0, 256), (0, 256, 256), (0, 512, 512), (0, 1024, 512), (0, 1536, 5
           (1, 0, 1024), (1, 1024, 1024), (1, 2048, 1024), (1, 3072, 1024)]
 MAX_CHUNK = 1024
 PIECE = 256
+VECTOR_PIECE_EVERY = 4
 CHUNK_LEAD = 10
 QUANTISE_WAIT = 2
 
 GROUP = 2
 MASK_STEP = 3
 SPLIT_FROM = N_TILES - 4
-SPLIT_EVERY = 4
-FIRST_SPLIT = 5
-SPLIT_TILES = list(range(FIRST_SPLIT, SPLIT_FROM, SPLIT_EVERY)) + list(range(SPLIT_FROM, N_TILES))
+SPLIT_EVERY = 8
+FIRST_SPLIT = 9
+SPREAD = [t for t in range(FIRST_SPLIT, SPLIT_FROM - 4, SPLIT_EVERY) if t % TILES_PER_IMAGE < TILES_PER_IMAGE - 6]
+SPLIT_TILES = SPREAD + list(range(SPLIT_FROM, N_TILES))
+POOL_LATER = 5
+POOL_ORDER = sorted(range(N_TILES), key=lambda t: t + (POOL_LATER + 0.5 if t in SPREAD else 0))
 HIGH_AFTER = 2
-LOW_AFTER = 4
+LOW_AFTER = 6
 POOL_AFTER = 6
-PRODUCT_BUFS = 5
+PRODUCT_BUFS = 6
 
 
 def regroup_begin(ci):
@@ -66,7 +70,7 @@ def tile_hydraattention_pa_t_kernel(tc, x, mask, W_kv, b_kv, out_0, out_1):
         const = ctx.enter_context(tc.tile_pool(name="const", bufs=1))
         stage = ctx.enter_context(tc.tile_pool(name="stage", bufs=2))
         work = ctx.enter_context(tc.tile_pool(name="work", bufs=3))
-        halves = ctx.enter_context(tc.tile_pool(name="halves", bufs=4))
+        halves = ctx.enter_context(tc.tile_pool(name="halves", bufs=5))
         products = ctx.enter_context(tc.tile_pool(name="products", bufs=PRODUCT_BUFS))
         psum_k = ctx.enter_context(tc.psum_pool(name="psum_k", bufs=3))
         psum_v = ctx.enter_context(tc.psum_pool(name="psum_v", bufs=4))
@@ -124,12 +128,12 @@ def tile_hydraattention_pa_t_kernel(tc, x, mask, W_kv, b_kv, out_0, out_1):
         def regroup(copy, dst, src):
             copy(out=dst.rearrange("p (c i) j -> p c j i", i=4), in_=src.rearrange("p j (c i) -> p c j i", i=4))
 
-        def regroup_piece(ci, n):
+        def regroup_piece(ci, n, copy):
             if n == 0:
                 x_grouped[ci] = stage.tile([P, MAX_CHUNK, PACK], BF16, align_bytes=64, tag="x_grouped",
                                            name="x_grouped")
             cols = slice(n * PIECE, (n + 1) * PIECE)
-            regroup(nc.scalar.copy, x_grouped[ci][:, cols, :], x_raw[ci][:, :, cols])
+            regroup(copy, x_grouped[ci][:, cols, :], x_raw[ci][:, :, cols])
 
         def quantise_chunk(ci):
             b, p0, width = CHUNKS[ci]
@@ -143,12 +147,12 @@ def tile_hydraattention_pa_t_kernel(tc, x, mask, W_kv, b_kv, out_0, out_1):
                                   in_=w_grouped[:, cols, :].rearrange("p w j -> p (w j)"))
 
         regroup(nc.vector.tensor_copy, w_grouped[:, 0:C, :], w_raw[0][:])
-        regroup_piece(0, 0)
+        regroup_piece(0, 0, nc.scalar.copy)
         regroup(nc.scalar.copy, w_grouped[:, C:C + C // 2, :], w_raw[1][:, :, 0:C // 2])
         quantise_w(0)
         quantise_chunk(0)
         regroup(nc.vector.tensor_copy, w_grouped[:, C + C // 2:2 * C, :], w_raw[1][:, :, C // 2:C])
-        regroup_piece(1, 0)
+        regroup_piece(1, 0, nc.scalar.copy)
         quantise_w(1)
 
         mask_f32 = const.tile([P, P], F32)
@@ -194,7 +198,7 @@ def tile_hydraattention_pa_t_kernel(tc, x, mask, W_kv, b_kv, out_0, out_1):
                                             rhs=w_codes[:, cols].bitcast(FP8X4), rhs_scale=w_scales[:, cols],
                                             start=True, stop=True)
                         if i > POOL_AFTER:
-                            pool_tile(i - POOL_AFTER - 1, range(2 * h + half, 2 * h + half + 1))
+                            pool_tile(POOL_ORDER[i - POOL_AFTER - 1], range(2 * h + half, 2 * h + half + 1))
                 if i % 2 == 0:
                     k_pair = work.tile([P, 2, C], F32, tag="k_pair")
                     v_pair = work.tile([P, 2, C], F32, tag="v_pair")
@@ -215,7 +219,11 @@ def tile_hydraattention_pa_t_kernel(tc, x, mask, W_kv, b_kv, out_0, out_1):
             for ci in range(1, len(CHUNKS)):
                 if i == quantise_step(ci):
                     quantise_chunk(ci)
-            if SPLIT_TILES[0] <= i - LOW_AFTER < SPLIT_FROM and i - LOW_AFTER in SPLIT_TILES:
+            for ci in range(len(CHUNKS)):
+                n = i - regroup_begin(ci)
+                if 0 <= n < CHUNKS[ci][2] // PIECE and i % VECTOR_PIECE_EVERY == 1:
+                    regroup_piece(ci, n, nc.vector.tensor_copy)
+            if i - LOW_AFTER in SPREAD:
                 low_part(i - LOW_AFTER)
             if i < N_TILES:
                 if i % 2 == 1:
@@ -228,13 +236,13 @@ def tile_hydraattention_pa_t_kernel(tc, x, mask, W_kv, b_kv, out_0, out_1):
                                                     op=ALU.mult)
                     product_of[i - 1] = product[:, 0, :]
                     product_of[i] = product[:, 1, :]
-            if i - HIGH_AFTER < SPLIT_FROM and i - HIGH_AFTER in SPLIT_TILES:
+            if i - HIGH_AFTER in SPREAD:
                 high_part(i - HIGH_AFTER)
             for ci in range(len(CHUNKS)):
                 n = i - regroup_begin(ci)
                 n_pieces = CHUNKS[ci][2] // PIECE
-                if 0 <= n < n_pieces:
-                    regroup_piece(ci, n)
+                if 0 <= n < n_pieces and i % VECTOR_PIECE_EVERY != 1:
+                    regroup_piece(ci, n, nc.scalar.copy)
             if i == 1:
                 nc.vector.tensor_copy(out=mask_f32[:], in_=mask_rows[:])
             if i == 2:
@@ -242,15 +250,19 @@ def tile_hydraattention_pa_t_kernel(tc, x, mask, W_kv, b_kv, out_0, out_1):
                 nc.tensor.transpose(mask_bank[:, 0:P], mask_f32[:], ident[:])
             if i == MASK_STEP:
                 nc.vector.tensor_copy(out=one_and_mask[:, :, 1], in_=mask_bank[:, 0:N_TILES])
-                n_spread = len(range(FIRST_SPLIT, SPLIT_FROM, SPLIT_EVERY))
-                nc.vector.tensor_copy(out=split_weights[:, 0:n_spread, 1], in_=mask_bank[:, FIRST_SPLIT:SPLIT_FROM:SPLIT_EVERY])
-                nc.vector.tensor_copy(out=split_weights[:, n_spread:, 1], in_=mask_bank[:, SPLIT_FROM:N_TILES])
+                half = sum(1 for t in SPREAD if t < TILES_PER_IMAGE)
+                for slots, first, step in ((slice(0, half), SPREAD[0], SPLIT_EVERY),
+                                           (slice(half, len(SPREAD)), SPREAD[half], SPLIT_EVERY),
+                                           (slice(len(SPREAD), len(SPLIT_TILES)), SPLIT_FROM, 1)):
+                    count = slots.stop - slots.start
+                    nc.vector.tensor_copy(out=split_weights[:, slots, 1],
+                                          in_=mask_bank[:, first:first + (count - 1) * step + 1:step])
             if i == N_TILES - 1:
                 for t in range(SPLIT_FROM, N_TILES):
                     high_part(t)
                     low_part(t)
             if i >= N_TILES:
-                pool_tile(i - POOL_AFTER - 1, range(C_BLOCKS))
+                pool_tile(POOL_ORDER[i - POOL_AFTER - 1], range(C_BLOCKS))
 
         for b in range(B):
             mask_sums = result[:, 8 + 4 * b:8 + 4 * (b + 1)]

@@ -27,11 +27,11 @@ CHUNKS = [(0, 0, 256), (0, 256, 256), (0, 512, 512), (0, 1024, 512), (0, 1536, 5
           (1, 0, 1024), (1, 1024, 1024), (1, 2048, 1024), (1, 3072, 1024)]
 MAX_CHUNK = 1024
 PIECE = 256
-VECTOR_PIECE_EVERY = 4
 CHUNK_LEAD = 10
 QUANTISE_WAIT = 2
 
 GROUP = 2
+SPLIT_WEIGHTS_STEP = 5
 MASK_STEP = 3
 SPLIT_FROM = N_TILES - 4
 SPLIT_EVERY = 8
@@ -90,21 +90,25 @@ def tile_hydraattention_pa_t_kernel(tc, x, mask, W_kv, b_kv, out_0, out_1):
             nc.sync.dma_start(out=x_raw[ci][:],
                               in_=x[b].rearrange("(p j) h w -> p j (h w)", j=PACK)[:, :, p0:p0 + width])
 
+        warm = const.tile([P, 1], F32)
+        nc.vector.memset(warm[:], 1.0)
+        nc.scalar.activation(out=warm[:], in_=warm[:], func=ACT.Abs_reciprocal_sqrt)
+        bias_row = const.tile([P, 2 * C], BF16)
+        nc.vector.memset(bias_row[:], 0.0)
         load_w(0)
         load_x(0)
+        nc.sync.dma_start(out=bias_row[0:1, :], in_=b_kv.unsqueeze(0))
         load_w(1)
         for ci in range(1, len(CHUNKS)):
             load_x(ci)
         bias_rows = const.tile([P, 2 * C], BF16)
-        nc.scalar.dma_start(out=bias_rows[:], in_=b_kv.partition_broadcast(P))
+        ones = const.tile([P, P], BF16)
+        nc.vector.memset(ones[:], 1.0)
         mask_rows = const.tile([P, P], BF16)
         nc.vector.memset(mask_rows[:], 0.0)
         nc.scalar.dma_start(out=mask_rows[0:N_TILES, :],
                             in_=mask.rearrange("b o (i h) w -> (b o i) (h w)", h=2))
 
-        warm = const.tile([P, 1], F32)
-        nc.vector.memset(warm[:], 1.0)
-        nc.scalar.activation(out=warm[:], in_=warm[:], func=ACT.Abs_reciprocal_sqrt)
         ident = const.tile([P, P], F32)
         make_identity(nc, ident[:])
         result = const.tile([P, P], F32)
@@ -146,9 +150,20 @@ def tile_hydraattention_pa_t_kernel(tc, x, mask, W_kv, b_kv, out_0, out_1):
             nc.vector.quantize_mx(out=w_codes[:, cols].bitcast(FP8X4), scales=w_scales[:, cols],
                                   in_=w_grouped[:, cols, :].rearrange("p w j -> p (w j)"))
 
+        bias_banks = []
+        for h, pool, tag in ((0, psum_k, "k_bank"), (1, psum_v, "v_bank")):
+            bank = pool.tile([P, C], F32, tag=tag, name="bias_bank%d" % h)
+            nc.tensor.matmul(out=bank[:], lhsT=ones[:], rhs=bias_row[:, h * C:(h + 1) * C], start=True, stop=True)
+            bias_banks.append(bank)
+
+        def spread_bias(h):
+            nc.scalar.copy(out=bias_rows[:, h * C:(h + 1) * C], in_=bias_banks[h][:])
+
         regroup(nc.vector.tensor_copy, w_grouped[:, 0:C, :], w_raw[0][:])
         regroup_piece(0, 0, nc.scalar.copy)
+        spread_bias(0)
         regroup(nc.scalar.copy, w_grouped[:, C:C + C // 2, :], w_raw[1][:, :, 0:C // 2])
+        spread_bias(1)
         quantise_w(0)
         quantise_chunk(0)
         regroup(nc.vector.tensor_copy, w_grouped[:, C + C // 2:2 * C, :], w_raw[1][:, :, C // 2:C])
@@ -156,6 +171,7 @@ def tile_hydraattention_pa_t_kernel(tc, x, mask, W_kv, b_kv, out_0, out_1):
         quantise_w(1)
 
         mask_f32 = const.tile([P, P], F32)
+        nc.gpsimd.tensor_copy(out=mask_f32[:], in_=mask_rows[:])
         norm_sq = const.tile([P, N_TILES], F32)
         inv_norm = const.tile([P, N_TILES], F32)
         pooled = psum_pool.tile([P, B, C_BLOCKS, POOL_COLS], F32)
@@ -206,23 +222,18 @@ def tile_hydraattention_pa_t_kernel(tc, x, mask, W_kv, b_kv, out_0, out_1):
                 squares = work.tile([P, C], BF16, tag="squares")
                 nc.scalar.activation(out=squares[:], in_=k_pair[:, i % 2, :], func=ACT.Square,
                                      accum_out=norm_sq[:, i:i + 1])
+            due = []
             for s in range(0, N_TILES, GROUP):
                 if i == max(s + GROUP - 1, MASK_STEP + 1):
                     nc.scalar.activation(out=inv_norm[:, s:s + GROUP], in_=norm_sq[:, s:s + GROUP],
                                          func=ACT.Abs_reciprocal_sqrt)
-                    for t in [t for t in range(s, s + GROUP) if t not in SPLIT_TILES]:
-                        nc.scalar.activation(out=weights[:, t, 0:2], in_=one_and_mask[:, t, :], func=ACT.Copy,
-                                             scale=inv_norm[:, t:t + 1])
+                    due.append(s)
             if i < N_TILES:
                 nc.vector.tensor_tensor(out=v_pair[:, i % 2, :], in0=v_bank[:], in1=bias_rows[:, C:2 * C],
                                         op=ALU.add)
             for ci in range(1, len(CHUNKS)):
                 if i == quantise_step(ci):
                     quantise_chunk(ci)
-            for ci in range(len(CHUNKS)):
-                n = i - regroup_begin(ci)
-                if 0 <= n < CHUNKS[ci][2] // PIECE and i % VECTOR_PIECE_EVERY == 1:
-                    regroup_piece(ci, n, nc.vector.tensor_copy)
             if i - LOW_AFTER in SPREAD:
                 low_part(i - LOW_AFTER)
             if i < N_TILES:
@@ -236,27 +247,30 @@ def tile_hydraattention_pa_t_kernel(tc, x, mask, W_kv, b_kv, out_0, out_1):
                                                     op=ALU.mult)
                     product_of[i - 1] = product[:, 0, :]
                     product_of[i] = product[:, 1, :]
+            for s in due:
+                nc.gpsimd.tensor_tensor(out=weights[:, s:s + GROUP, 0:2], in0=one_and_mask[:, s:s + GROUP, :],
+                                        in1=inv_norm[:, s:s + GROUP].unsqueeze(2).to_broadcast([P, GROUP, 2]),
+                                        op=ALU.mult)
             if i - HIGH_AFTER in SPREAD:
                 high_part(i - HIGH_AFTER)
             for ci in range(len(CHUNKS)):
                 n = i - regroup_begin(ci)
                 n_pieces = CHUNKS[ci][2] // PIECE
-                if 0 <= n < n_pieces and i % VECTOR_PIECE_EVERY != 1:
+                if 0 <= n < n_pieces:
                     regroup_piece(ci, n, nc.scalar.copy)
-            if i == 1:
-                nc.vector.tensor_copy(out=mask_f32[:], in_=mask_rows[:])
             if i == 2:
                 mask_bank = psum_k.tile([P, C], F32, tag="k_bank", name="mask_bank")
                 nc.tensor.transpose(mask_bank[:, 0:P], mask_f32[:], ident[:])
             if i == MASK_STEP:
-                nc.vector.tensor_copy(out=one_and_mask[:, :, 1], in_=mask_bank[:, 0:N_TILES])
+                nc.scalar.copy(out=one_and_mask[:, :, 1], in_=mask_bank[:, 0:N_TILES])
+            if i == SPLIT_WEIGHTS_STEP:
                 half = sum(1 for t in SPREAD if t < TILES_PER_IMAGE)
                 for slots, first, step in ((slice(0, half), SPREAD[0], SPLIT_EVERY),
                                            (slice(half, len(SPREAD)), SPREAD[half], SPLIT_EVERY),
                                            (slice(len(SPREAD), len(SPLIT_TILES)), SPLIT_FROM, 1)):
                     count = slots.stop - slots.start
-                    nc.vector.tensor_copy(out=split_weights[:, slots, 1],
-                                          in_=mask_bank[:, first:first + (count - 1) * step + 1:step])
+                    nc.gpsimd.tensor_copy(out=split_weights[:, slots, 1],
+                                          in_=one_and_mask[:, first:first + (count - 1) * step + 1:step, 1])
             if i == N_TILES - 1:
                 for t in range(SPLIT_FROM, N_TILES):
                     high_part(t)

@@ -27,6 +27,7 @@ CHUNKS = [(0, 0, 256), (0, 256, 256), (0, 512, 512), (0, 1024, 512), (0, 1536, 5
           (1, 0, 1024), (1, 1024, 1024), (1, 2048, 1024), (1, 3072, 1024)]
 MAX_CHUNK = 1024
 PIECE = 256
+VECTOR_PIECE_STEPS = range(9, N_TILES, 16)
 CHUNK_LEAD = 10
 QUANTISE_WAIT = 2
 
@@ -222,18 +223,23 @@ def tile_hydraattention_pa_t_kernel(tc, x, mask, W_kv, b_kv, out_0, out_1):
                 squares = work.tile([P, C], BF16, tag="squares")
                 nc.scalar.activation(out=squares[:], in_=k_pair[:, i % 2, :], func=ACT.Square,
                                      accum_out=norm_sq[:, i:i + 1])
-            due = []
             for s in range(0, N_TILES, GROUP):
                 if i == max(s + GROUP - 1, MASK_STEP + 1):
                     nc.scalar.activation(out=inv_norm[:, s:s + GROUP], in_=norm_sq[:, s:s + GROUP],
                                          func=ACT.Abs_reciprocal_sqrt)
-                    due.append(s)
+                    for t in [t for t in range(s, s + GROUP) if t not in SPLIT_TILES]:
+                        nc.scalar.activation(out=weights[:, t, 0:2], in_=one_and_mask[:, t, :], func=ACT.Copy,
+                                             scale=inv_norm[:, t:t + 1])
             if i < N_TILES:
                 nc.vector.tensor_tensor(out=v_pair[:, i % 2, :], in0=v_bank[:], in1=bias_rows[:, C:2 * C],
                                         op=ALU.add)
             for ci in range(1, len(CHUNKS)):
                 if i == quantise_step(ci):
                     quantise_chunk(ci)
+            for ci in range(len(CHUNKS)):
+                n = i - regroup_begin(ci)
+                if 0 <= n < CHUNKS[ci][2] // PIECE and i in VECTOR_PIECE_STEPS:
+                    regroup_piece(ci, n, nc.vector.tensor_copy)
             if i - LOW_AFTER in SPREAD:
                 low_part(i - LOW_AFTER)
             if i < N_TILES:
@@ -247,16 +253,12 @@ def tile_hydraattention_pa_t_kernel(tc, x, mask, W_kv, b_kv, out_0, out_1):
                                                     op=ALU.mult)
                     product_of[i - 1] = product[:, 0, :]
                     product_of[i] = product[:, 1, :]
-            for s in due:
-                nc.gpsimd.tensor_tensor(out=weights[:, s:s + GROUP, 0:2], in0=one_and_mask[:, s:s + GROUP, :],
-                                        in1=inv_norm[:, s:s + GROUP].unsqueeze(2).to_broadcast([P, GROUP, 2]),
-                                        op=ALU.mult)
             if i - HIGH_AFTER in SPREAD:
                 high_part(i - HIGH_AFTER)
             for ci in range(len(CHUNKS)):
                 n = i - regroup_begin(ci)
                 n_pieces = CHUNKS[ci][2] // PIECE
-                if 0 <= n < n_pieces:
+                if 0 <= n < n_pieces and i not in VECTOR_PIECE_STEPS:
                     regroup_piece(ci, n, nc.scalar.copy)
             if i == 2:
                 mask_bank = psum_k.tile([P, C], F32, tag="k_bank", name="mask_bank")

@@ -214,8 +214,11 @@ def tile_hydraattention_pa_t_kernel(tc, x, mask, W_kv, b_kv, out_0, out_1):
                                             lhsT=x_codes[:, pixels].bitcast(FP8X4), lhsT_scale=x_scales[:, pixels],
                                             rhs=w_codes[:, cols].bitcast(FP8X4), rhs_scale=w_scales[:, cols],
                                             start=True, stop=True)
-                        if i > POOL_AFTER:
-                            pool_tile(POOL_ORDER[i - POOL_AFTER - 1], range(2 * h + half, 2 * h + half + 1))
+                        t = POOL_ORDER[i - POOL_AFTER - 1] if i > POOL_AFTER else None
+                        if t is not None and t not in SPREAD:
+                            pool_tile(t, range(2 * h + half, 2 * h + half + 1))
+                if t is not None and t in SPREAD:
+                    pool_tile(t, range(C_BLOCKS))
                 if i % 2 == 0:
                     k_pair = work.tile([P, 2, C], F32, tag="k_pair")
                     v_pair = work.tile([P, 2, C], F32, tag="v_pair")

from contextlib import ExitStack

import concourse.mybir as mybir
from concourse.masks import make_identity

F32 = mybir.dt.float32
BF16 = mybir.dt.bfloat16
U32 = mybir.dt.uint32
U8 = mybir.dt.uint8
FP8X4 = mybir.dt.float8_e4m3fn_x4
ALU = mybir.AluOpType
ACT = mybir.ActivationFunctionType

P = 128
PACK = 4
B = 2
C = 512
T = 4096
N_TILES = B * T // P
TILES_PER_IMAGE = T // P
C_BLOCKS = C // P
FLOPS = 2 * B * T * C * (2 * C)

POOL_COLS = 64

CHUNKS = [(0, 0, 256), (0, 256, 256), (0, 512, 512), (0, 1024, 512), (0, 1536, 512), (0, 2048, 1024), (0, 3072, 1024),
          (1, 0, 1024), (1, 1024, 1024), (1, 2048, 1024), (1, 3072, 1024)]
MAX_CHUNK = 1024
PIECE = 256
VECTOR_PIECE_STEPS = range(9, N_TILES, 16)
CHUNK_LEAD = 10
QUANTISE_WAIT = 2

GROUP = 2
SPLIT_WEIGHTS_STEP = 5
MASK_STEP = 3
SPLIT_FROM = N_TILES - 4
SPLIT_EVERY = 8
FIRST_SPLIT = 9
SPREAD = [t for t in range(FIRST_SPLIT, SPLIT_FROM - 4, SPLIT_EVERY) if t % TILES_PER_IMAGE < TILES_PER_IMAGE - 6]
SPLIT_TILES = SPREAD + list(range(SPLIT_FROM, N_TILES))
POOL_LATER = 5
POOL_ORDER = sorted(range(N_TILES), key=lambda t: t + (POOL_LATER + 0.5 if t in SPREAD else 0))
HIGH_AFTER = 2
LOW_AFTER = 6
POOL_AFTER = 6
PRODUCT_BUFS = 6


def regroup_begin(ci):
    b, p0, width = CHUNKS[ci]
    first_pixel = b * T + p0
    return max(first_pixel // PIECE - 2, first_pixel // P - CHUNK_LEAD)


def quantise_step(ci):
    b, p0, width = CHUNKS[ci]
    in_time = regroup_begin(ci) == (b * T + p0) // P - CHUNK_LEAD
    step = regroup_begin(ci) + width // PIECE + (QUANTISE_WAIT if in_time else 0)
    return step + 1 - step % 2


def group_due(step, distance):
    last = step - distance
    return last - (GROUP - 1) if 0 <= last < N_TILES and last % GROUP == GROUP - 1 else None


def tile_hydraattention_pa_t_kernel(tc, x, mask, W_kv, b_kv, out_0, out_1):
    nc = tc.nc
    with ExitStack() as ctx:
        const = ctx.enter_context(tc.tile_pool(name="const", bufs=1))
        stage = ctx.enter_context(tc.tile_pool(name="stage", bufs=2))
        work = ctx.enter_context(tc.tile_pool(name="work", bufs=3))
        halves = ctx.enter_context(tc.tile_pool(name="halves", bufs=5))
        products = ctx.enter_context(tc.tile_pool(name="products", bufs=PRODUCT_BUFS))
        psum_k = ctx.enter_context(tc.psum_pool(name="psum_k", bufs=3))
        psum_v = ctx.enter_context(tc.psum_pool(name="psum_v", bufs=4))
        psum_pool = ctx.enter_context(tc.psum_pool(name="psum_pool", bufs=1))
        ctx.enter_context(tc.manual_schedule())

        w_raw = [const.tile([P, PACK, C], BF16, name="w_raw%d" % h) for h in range(2)]
        x_raw = [const.tile([P, PACK, width], BF16, name="x_raw%d" % ci)
                 for ci, (b, p0, width) in enumerate(CHUNKS)]

        def load_w(h):
            nc.sync.dma_start(out=w_raw[h][:],
                              in_=W_kv.rearrange("(p j) n -> p j n", j=PACK)[:, :, h * C:(h + 1) * C])

        def load_x(ci):
            b, p0, width = CHUNKS[ci]
            nc.sync.dma_start(out=x_raw[ci][:],
                              in_=x[b].rearrange("(p j) h w -> p j (h w)", j=PACK)[:, :, p0:p0 + width])

        warm = const.tile([P, 1], F32)
        nc.vector.memset(warm[:], 1.0)
        nc.scalar.activation(out=warm[:], in_=warm[:], func=ACT.Abs_reciprocal_sqrt)
        bias_row = const.tile([P, 2 * C], BF16)
        nc.vector.memset(bias_row[:], 0.0)
        load_w(0)
        load_x(0)
        nc.sync.dma_start(out=bias_row[0:1, :], in_=b_kv.unsqueeze(0))
        load_w(1)
        for ci in range(1, len(CHUNKS)):
            load_x(ci)
        bias_rows = const.tile([P, 2 * C], BF16)
        ones = const.tile([P, P], BF16)
        nc.vector.memset(ones[:], 1.0)
        mask_rows = const.tile([P, P], BF16)
        nc.vector.memset(mask_rows[:], 0.0)
        nc.scalar.dma_start(out=mask_rows[0:N_TILES, :],
                            in_=mask.rearrange("b o (i h) w -> (b o i) (h w)", h=2))

        ident = const.tile([P, P], F32)
        make_identity(nc, ident[:])
        result = const.tile([P, P], F32)
        nc.vector.memset(result[:], 0.0)
        weights = const.tile([P, N_TILES, POOL_COLS], F32)
        nc.gpsimd.memset(weights[:], 0.0)

        one_and_mask = const.tile([P, N_TILES, 2], F32)
        nc.vector.memset(one_and_mask[:], 1.0)
        split_weights = const.tile([P, len(SPLIT_TILES), POOL_COLS], BF16)
        nc.vector.memset(split_weights[:], 0.0)
        nc.vector.memset(split_weights[:, :, 0:1], 1.0)

        w_grouped = const.tile([P, 2 * C, PACK], BF16, align_bytes=64)
        w_codes = const.tile([P, 2 * C], U32, align_bytes=64)
        w_scales = const.tile([P, 2 * C], U8, align_bytes=64)
        x_codes = const.tile([P, B * T], U32, align_bytes=64)
        x_scales = const.tile([P, B * T], U8, align_bytes=64)
        x_grouped = {}

        def regroup(copy, dst, src):
            copy(out=dst.rearrange("p (c i) j -> p c j i", i=4), in_=src.rearrange("p j (c i) -> p c j i", i=4))

        def regroup_piece(ci, n, copy):
            if n == 0:
                x_grouped[ci] = stage.tile([P, MAX_CHUNK, PACK], BF16, align_bytes=64, tag="x_grouped",
                                           name="x_grouped")
            cols = slice(n * PIECE, (n + 1) * PIECE)
            regroup(copy, x_grouped[ci][:, cols, :], x_raw[ci][:, :, cols])

        def quantise_chunk(ci):
            b, p0, width = CHUNKS[ci]
            cols = slice(b * T + p0, b * T + p0 + width)
            nc.vector.quantize_mx(out=x_codes[:, cols].bitcast(FP8X4), scales=x_scales[:, cols],
                                  in_=x_grouped[ci][:, 0:width, :].rearrange("p w j -> p (w j)"))

        def quantise_w(h):
            cols = slice(h * C, (h + 1) * C)
            nc.vector.quantize_mx(out=w_codes[:, cols].bitcast(FP8X4), scales=w_scales[:, cols],
                                  in_=w_grouped[:, cols, :].rearrange("p w j -> p (w j)"))

        bias_banks = []
        for h, pool, tag in ((0, psum_k, "k_bank"), (1, psum_v, "v_bank")):
            bank = pool.tile([P, C], F32, tag=tag, name="bias_bank%d" % h)
            nc.tensor.matmul(out=bank[:], lhsT=ones[:], rhs=bias_row[:, h * C:(h + 1) * C], start=True, stop=True)
            bias_banks.append(bank)

        def spread_bias(h):
            nc.scalar.copy(out=bias_rows[:, h * C:(h + 1) * C], in_=bias_banks[h][:])

        regroup(nc.vector.tensor_copy, w_grouped[:, 0:C, :], w_raw[0][:])
        regroup_piece(0, 0, nc.scalar.copy)
        spread_bias(0)
        regroup(nc.scalar.copy, w_grouped[:, C:C + C // 2, :], w_raw[1][:, :, 0:C // 2])
        spread_bias(1)
        quantise_w(0)
        quantise_chunk(0)
        regroup(nc.vector.tensor_copy, w_grouped[:, C + C // 2:2 * C, :], w_raw[1][:, :, C // 2:C])
        regroup_piece(1, 0, nc.scalar.copy)
        quantise_w(1)

        mask_f32 = const.tile([P, P], F32)
        nc.gpsimd.tensor_copy(out=mask_f32[:], in_=mask_rows[:])
        norm_sq = const.tile([P, N_TILES], F32)
        inv_norm = const.tile([P, N_TILES], F32)
        pooled = psum_pool.tile([P, B, C_BLOCKS, POOL_COLS], F32)
        product_of = {}
        split_of = {}

        def pool_tile(t, blocks):
            b = t // TILES_PER_IMAGE
            parts = split_of[t] if t in SPLIT_TILES else [product_of[t]]
            rhs = split_weights[:, SPLIT_TILES.index(t), :] if t in SPLIT_TILES else weights[:, t, :]
            for q in blocks:
                for part in parts:
                    nc.tensor.matmul(out=pooled[:, b, q, :], lhsT=part[:, q * P:(q + 1) * P], rhs=rhs,
                                     start=(t % TILES_PER_IMAGE == 0 and q == 0),
                                     stop=(t % TILES_PER_IMAGE == TILES_PER_IMAGE - 1 and q == C_BLOCKS - 1
                                           and part is parts[-1]))

        def high_part(t):
            high = halves.tile([P, C], BF16, tag="high")
            nc.scalar.activation(out=high[:], in_=product_of[t], func=ACT.Copy, scale=inv_norm[:, t:t + 1])
            split_of[t] = [high]

        def low_part(t):
            high = split_of[t][0]
            low = halves.tile([P, C], BF16, tag="low")
            nc.vector.scalar_tensor_tensor(out=low[:], in0=product_of[t], scalar=inv_norm[:, t:t + 1], in1=high[:],
                                           op0=ALU.mult, op1=ALU.subtract)
            split_of[t].append(low)

        for i in range(N_TILES + POOL_AFTER + 1):
            if i < N_TILES:
                pixels = slice(i * P, (i + 1) * P)
                k_bank = psum_k.tile([P, C], F32, tag="k_bank")
                v_bank = psum_v.tile([P, C], F32, tag="v_bank")
                for h, bank in ((0, k_bank), (1, v_bank)):
                    for half in range(2):
                        cols = slice(h * C + half * (C // 2), h * C + (half + 1) * (C // 2))
                        nc.tensor.matmul_mx(out=bank[:, half * (C // 2):(half + 1) * (C // 2)],
                                            lhsT=x_codes[:, pixels].bitcast(FP8X4), lhsT_scale=x_scales[:, pixels],
                                            rhs=w_codes[:, cols].bitcast(FP8X4), rhs_scale=w_scales[:, cols],
                                            start=True, stop=True)
                        t = POOL_ORDER[i - POOL_AFTER - 1] if i > POOL_AFTER else None
                        if t is not None and t not in SPREAD:
                            pool_tile(t, range(2 * h + half, 2 * h + half + 1))
                if t is not None and t in SPREAD:
                    pool_tile(t, range(C_BLOCKS))
                if i % 2 == 0:
                    k_pair = work.tile([P, 2, C], F32, tag="k_pair")
                    v_pair = work.tile([P, 2, C], F32, tag="v_pair")
                nc.vector.tensor_tensor(out=k_pair[:, i % 2, :], in0=k_bank[:], in1=bias_rows[:, 0:C], op=ALU.add)
                squares = work.tile([P, C], BF16, tag="squares")
                nc.scalar.activation(out=squares[:], in_=k_pair[:, i % 2, :], func=ACT.Square,
                                     accum_out=norm_sq[:, i:i + 1])
            for s in range(0, N_TILES, GROUP):
                if i == max(s + GROUP - 1, MASK_STEP + 1):
                    nc.scalar.activation(out=inv_norm[:, s:s + GROUP], in_=norm_sq[:, s:s + GROUP],
                                         func=ACT.Abs_reciprocal_sqrt)
                    for t in [t for t in range(s, s + GROUP) if t not in SPLIT_TILES]:
                        nc.scalar.activation(out=weights[:, t, 0:2], in_=one_and_mask[:, t, :], func=ACT.Copy,
                                             scale=inv_norm[:, t:t + 1])
            if i < N_TILES:
                nc.vector.tensor_tensor(out=v_pair[:, i % 2, :], in0=v_bank[:], in1=bias_rows[:, C:2 * C],
                                        op=ALU.add)
            for ci in range(1, len(CHUNKS)):
                if i == quantise_step(ci):
                    quantise_chunk(ci)
            for ci in range(len(CHUNKS)):
                n = i - regroup_begin(ci)
                if 0 <= n < CHUNKS[ci][2] // PIECE and i in VECTOR_PIECE_STEPS:
                    regroup_piece(ci, n, nc.vector.tensor_copy)
            if i - LOW_AFTER in SPREAD:
                low_part(i - LOW_AFTER)
            if i < N_TILES:
                if i % 2 == 1:
                    product = products.tile([P, 2, C], F32, tag="product")
                    if i < N_TILES - 1:
                        nc.gpsimd.tensor_tensor(out=product[:], in0=k_pair[:], in1=v_pair[:], op=ALU.mult)
                    else:
                        for e in range(2):
                            nc.vector.tensor_tensor(out=product[:, e, :], in0=k_pair[:, e, :], in1=v_pair[:, e, :],
                                                    op=ALU.mult)
                    product_of[i - 1] = product[:, 0, :]
                    product_of[i] = product[:, 1, :]
            if i - HIGH_AFTER in SPREAD:
                high_part(i - HIGH_AFTER)
            for ci in range(len(CHUNKS)):
                n = i - regroup_begin(ci)
                n_pieces = CHUNKS[ci][2] // PIECE
                if 0 <= n < n_pieces and i not in VECTOR_PIECE_STEPS:
                    regroup_piece(ci, n, nc.scalar.copy)
            if i == 2:
                mask_bank = psum_k.tile([P, C], F32, tag="k_bank", name="mask_bank")
                nc.tensor.transpose(mask_bank[:, 0:P], mask_f32[:], ident[:])
            if i == MASK_STEP:
                nc.scalar.copy(out=one_and_mask[:, :, 1], in_=mask_bank[:, 0:N_TILES])
            if i == SPLIT_WEIGHTS_STEP:
                half = sum(1 for t in SPREAD if t < TILES_PER_IMAGE)
                for slots, first, step in ((slice(0, half), SPREAD[0], SPLIT_EVERY),
                                           (slice(half, len(SPREAD)), SPREAD[half], SPLIT_EVERY),
                                           (slice(len(SPREAD), len(SPLIT_TILES)), SPLIT_FROM, 1)):
                    count = slots.stop - slots.start
                    nc.gpsimd.tensor_copy(out=split_weights[:, slots, 1],
                                          in_=one_and_mask[:, first:first + (count - 1) * step + 1:step, 1])
            if i == N_TILES - 1:
                for t in range(SPLIT_FROM, N_TILES):
                    high_part(t)
                    low_part(t)
            if i >= N_TILES:
                pool_tile(POOL_ORDER[i - POOL_AFTER - 1], range(C_BLOCKS))

        for b in range(B):
            mask_sums = result[:, 8 + 4 * b:8 + 4 * (b + 1)]
            nc.vector.tensor_copy(out=mask_sums, in_=pooled[:, b, :, 1])
            nc.vector.tensor_tensor(out=result[:, 4 * b:4 * (b + 1)], in0=pooled[:, b, :, 0], in1=mask_sums,
                                    op=ALU.subtract)
        result_bank = psum_k.tile([P, C], F32, tag="k_bank", name="result_bank")
        nc.tensor.transpose(result_bank[:, 0:P], result[:], ident[:])
        result_rows = const.tile([16, P], F32)
        nc.scalar.copy(out=result_rows[:], in_=result_bank[0:16, 0:P])
        nc.sync.dma_start(out=out_0.rearrange("b o (q p) -> (b o q) p", p=P), in_=result_rows[0:8, :])
        nc.sync.dma_start(out=out_1.rearrange("b o (q p) -> (b o q) p", p=P), in_=result_rows[8:16, :])
